import numpy as np
import ml_dtypes


def mxq(x, axis, fmt="e4m3"):
    dtype, down = {"e4m3": (ml_dtypes.float8_e4m3fn, 7), "e5m2": (ml_dtypes.float8_e5m2, 14)}[fmt]
    v = np.moveaxis(np.asarray(x, np.float32).astype(ml_dtypes.bfloat16).astype(np.float64), axis, -1)
    blocks = v.reshape(v.shape[:-1] + (-1, 32))
    amax = np.abs(blocks).max(-1, keepdims=True)
    byte = np.maximum(np.where(amax > 0, np.frexp(amax)[1] - 1 + 127, 0) - down, 1)
    scale = np.exp2(byte - 127.0)
    codes = (blocks / scale).astype(np.float32).astype(dtype).astype(np.float64)
    return np.moveaxis((codes * scale).reshape(v.shape), -1, axis)


WIDE = False


def mx_kscale(k):
    if not WIDE:
        return np.ones(k)
    levels = np.array([20, -20, 10, -10, 0])
    a = np.random.permutation(np.resize(levels, k // 512 * 4)).reshape(k // 512, 4)
    idx = np.arange(k)
    return np.exp2(a[idx // 512, idx % 128 // 32])


BF16 = ml_dtypes.bfloat16


def bf(x):
    return np.asarray(x, np.float32).astype(BF16)


def f64(x):
    return np.asarray(x).astype(np.float64)


B, IN, OUT, CHEBY_ORDER = 1024, 512, 512, 10


def sigmoid(v):
    return 1.0 / (1.0 + np.exp(-v))


def silu(v):
    return v * sigmoid(v)


def dsilu(v):
    s = sigmoid(v)
    return s * (1.0 + v * (1.0 - s))


def chebyshev_bases(x, order):
    t0 = np.ones_like(x)
    if order == 1:
        return t0[None]
    ts = [t0, x]
    for _ in range(2, order):
        ts.append(2.0 * x * ts[-1] - ts[-2])
    return np.stack(ts)


def chebyshev_derivs(x, order):
    ts = chebyshev_bases(x, order)
    d0 = np.zeros_like(x)
    if order == 1:
        return d0[None]
    ds = [d0, np.ones_like(x)]
    for n in range(2, order):
        ds.append(2.0 * ts[n - 1] + 2.0 * x * ds[-1] - ds[-2])
    return np.stack(ds)


def setup_inputs():
    u = mx_kscale(OUT)
    x = np.random.random_sample((B, IN))
    base_weight = np.random.standard_normal((OUT, IN)) * 0.05 / u[:, None]
    cheby_weight = np.random.standard_normal((OUT, IN, CHEBY_ORDER)) * 0.05 / u[:, None, None]
    g = np.random.standard_normal((B, OUT)) * np.exp2(np.random.randint(-12, 1, (B, 1))) * 4.0 * u
    return {"x": bf(x), "base_weight": bf(base_weight), "cheby_weight": bf(cheby_weight), "grad_out": bf(g)}


def reference(x, base_weight, cheby_weight, grad_out):
    x = f64(x)
    base_weight = f64(base_weight)
    cheby_weight = f64(cheby_weight)
    b, n_in = x.shape
    n_out, _, o = cheby_weight.shape
    gq = mxq(f64(grad_out), 1, "e5m2")
    a = gq @ mxq(base_weight, 0, "e4m3")
    w = cheby_weight.reshape(n_out, n_in * o)
    d_flat = (gq @ mxq(w, 0, "e4m3")) / o
    d_bases = d_flat.reshape(o, b, n_in)
    return a * dsilu(x) + (d_bases * chebyshev_derivs(x, o)).sum(axis=0)

@@ -1,0 +1,290 @@
+import math
+from contextlib import ExitStack
+
+import concourse.mybir as mybir
+from concourse.masks import make_identity
+
+F32 = mybir.dt.float32
+BF16 = mybir.dt.bfloat16
+U32 = mybir.dt.uint32
+U8 = mybir.dt.uint8
+E4 = mybir.dt.float8_e4m3fn_x4
+E5 = mybir.dt.float8_e5m2_x4
+ALU = mybir.AluOpType
+ACT = mybir.ActivationFunctionType
+
+FLOPS = 2 * 1024 * 512 * 5632
+
+P = 128
+J = 104
+PL = 10 * J
+EP = 5 * PL + 32
+LAM = 0.375
+
+
+def theta(n):
+    return (4 * n) % 10
+
+
+def seg_start(n):
+    return (1024 * n - theta(n)) // 10
+
+
+def seg_addr(n, c):
+    t = theta(n)
+    if c >= t:
+        return J * (c - t)
+    return J * (c - t + 10) - 1
+
+
+def tile_kantlinear_kernel(tc, x, base_weight, cheby_weight, grad_out, out):
+    nc = tc.nc
+    with ExitStack() as ctx:
+        const = ctx.enter_context(tc.tile_pool(name="const", bufs=1))
+        rawp = ctx.enter_context(tc.tile_pool(name="rawp", bufs=3))
+        grpp = ctx.enter_context(tc.tile_pool(name="grpp", bufs=3))
+        keep = ctx.enter_context(tc.tile_pool(name="keep", bufs=1))
+        wqp = ctx.enter_context(tc.tile_pool(name="wqp", bufs=2))
+        upl = ctx.enter_context(tc.tile_pool(name="upl", bufs=2))
+        hlp = ctx.enter_context(tc.tile_pool(name="hlp", bufs=1))
+        otp = ctx.enter_context(tc.tile_pool(name="otp", bufs=2))
+        pmx = ctx.enter_context(tc.psum_pool(name="pmx", bufs=4))
+        ptr = ctx.enter_context(tc.psum_pool(name="ptr", bufs=2))
+        pac = ctx.enter_context(tc.psum_pool(name="pac", bufs=2))
+
+        ident_f = const.tile([P, P], F32, name="ident_f")
+        make_identity(nc, ident_f[:])
+        ident_b = const.tile([P, P], BF16, name="ident_b")
+        make_identity(nc, ident_b[:])
+
+        gs = rawp.tile([P, 8, 512], BF16, name="gs", tag="raw")
+        nc.sync.dma_start(out=gs[:], in_=grad_out.rearrange("(t p) k -> p t k", p=P))
+        xs = rawp.tile([P, 10, 512], BF16, name="xs", tag="raw")
+        nc.gpsimd.memset(xs[96:128], 0.0)
+        nc.sync.dma_start(out=xs[0:96], in_=x[0:960, :].rearrange("(j r) i -> j r i", r=10))
+        nc.sync.dma_start(out=xs[96:102], in_=x[960:1020, :].rearrange("(j r) i -> j r i", r=10))
+        nc.sync.dma_start(out=xs[102:103, 0:4, :], in_=x[1020:1024, :].rearrange("(o r) i -> o r i", o=1))
+        braw = rawp.tile([P, 4, 512], BF16, name="braw", tag="raw")
+        nc.sync.dma_start(
+            out=braw[:].rearrange("p (u e) n -> p u e n", u=2),
+            in_=base_weight.rearrange("(u q e) n -> q u e n", u=2, e=2),
+        )
+        w4 = cheby_weight.rearrange("o i k -> o (i k)").rearrange("(u q e) n -> q u e n", u=2, e=2)
+
+        def load_w(it):
+            raw = rawp.tile([P, 4, 1280], BF16, name="raw", tag="raw")
+            for t in range(4):
+                nc.sync.dma_start(
+                    out=raw[:, t, :].rearrange("p (c f) -> p c f", c=10),
+                    in_=w4[:, t // 2, t % 2, :].rearrange("q (c f) -> q c f", c=10)[:, :, it * P : (it + 1) * P],
+                )
+            return raw
+
+        def regroup(dst, src, c0, c1, eng):
+            d = dst[:, c0:c1, :].rearrange("p (c i) t -> p c t i", i=4)
+            s = src[:, :, c0:c1].rearrange("p t (c i) -> p c t i", i=4)
+            if eng == "v":
+                nc.vector.tensor_copy(out=d, in_=s)
+            else:
+                nc.scalar.copy(out=d, in_=s)
+
+        gn = grpp.tile([P, 1032, 4], BF16, name="gn", tag="grp", align_bytes=64)
+        gn32 = gn[:].bitcast(F32)
+        gs32 = gs[:].bitcast(F32)
+        nc.vector.memset(gn32[:, 1024:1032, :], 0.0)
+        for q in range(4):
+            pt = ptr.tile([P, 2, 256], F32, name="ptg", tag="tr")
+            for b in range(2):
+                for u in range(2):
+                    nc.tensor.transpose(
+                        pt[:, u, b * P : (b + 1) * P], gs32[:, 2 * q + b, u * P : (u + 1) * P], ident_f[:]
+                    )
+            nc.scalar.copy(out=gn32[:, 256 * q : 256 * q + 256, :], in_=pt[:].rearrange("p u r -> p r u"))
+        gw = grpp.tile([P, 1024, 4], BF16, name="gw", tag="grp", align_bytes=64)
+        gw32 = gw[:].bitcast(F32)
+        for wi, ns in enumerate(((1, 6, 2, 7), (3, 8, 4, 9))):
+            for k, n in enumerate(ns):
+                s = seg_start(n)
+                nc.vector.tensor_copy(
+                    out=gw32[:, 512 * wi + J * k : 512 * wi + J * k + J, :], in_=gn32[:, s : s + J, :]
+                )
+            nc.vector.tensor_copy(
+                out=gw32[:, 512 * wi + 416 : 512 * wi + 468, :], in_=gn32[:, 512 + 52 * wi : 564 + 52 * wi, :]
+            )
+            nc.vector.memset(gw32[:, 512 * wi + 468 : 512 * wi + 512, :], 0.0)
+        gcodes = keep.tile([P, 2048], U32, name="gcodes", align_bytes=64)
+        gscales = keep.tile([P, 2048], U8, name="gscales", align_bytes=64)
+        nc.vector.quantize_mx(
+            out=gcodes[:, 0:1024].bitcast(E5),
+            scales=gscales[:, 0:1024],
+            in_=gn[:, 0:1024, :].rearrange("p r t -> p (r t)"),
+        )
+        nc.vector.quantize_mx(
+            out=gcodes[:, 1024:2048].bitcast(E5),
+            scales=gscales[:, 1024:2048],
+            in_=gw[:].rearrange("p r t -> p (r t)"),
+        )
+
+        xT = keep.tile([P, 40, J], BF16, name="xT")
+        for grp in range(5):
+            pt = ptr.tile([P, 8, P], BF16, name="ptx", tag="tr")
+            for k in range(8):
+                it, beta = divmod(8 * grp + k, 10)
+                nc.tensor.transpose(pt[:, k, :], xs[:, beta, it * P : (it + 1) * P], ident_b[:])
+            nc.scalar.copy(out=xT[:, 8 * grp : 8 * grp + 8, :], in_=pt[:, :, 0:J])
+
+        bgrp = grpp.tile([P, 512, 4], BF16, name="bgrp", tag="grp", align_bytes=64)
+        regroup(bgrp, braw, 0, 512, "v")
+        bcodes = keep.tile([P, 512], U32, name="bcodes", align_bytes=64)
+        bscales = keep.tile([P, 512], U8, name="bscales", align_bytes=64)
+        nc.vector.quantize_mx(
+            out=bcodes[:].bitcast(E4), scales=bscales[:], in_=bgrp[:].rearrange("p r t -> p (r t)")
+        )
+
+        def prep_w(it):
+            raw = load_w(it)
+            grp = grpp.tile([P, 1280, 4], BF16, name="grp", tag="grp", align_bytes=64)
+            regroup(grp, raw, 0, 512, "v")
+            regroup(grp, raw, 512, 1024, "s")
+            regroup(grp, raw, 1024, 1280, "s")
+            wc = wqp.tile([P, 1280], U32, name="wc", align_bytes=64)
+            ws = wqp.tile([P, 1280], U8, name="ws", align_bytes=64)
+            nc.vector.quantize_mx(
+                out=wc[:, 0:1024].bitcast(E4),
+                scales=ws[:, 0:1024],
+                in_=grp[:, 0:1024, :].rearrange("p r t -> p (r t)"),
+            )
+            nc.vector.quantize_mx(
+                out=wc[:, 1024:1280].bitcast(E4),
+                scales=ws[:, 1024:1280],
+                in_=grp[:, 1024:1280, :].rearrange("p r t -> p (r t)"),
+            )
+            return wc, ws
+
+        def basis(it):
+            u = upl.tile([P, 2, EP], F32, name="u")
+
+            def pl(n):
+                return u[:, n // 5, (n % 5) * PL : (n % 5) * PL + PL]
+
+            xv = xT[:, 10 * it : 10 * it + 10, :].rearrange("p b j -> p (b j)")
+            nc.gpsimd.memset(u[:, :, 5 * PL : EP], 0.0)
+            nc.gpsimd.memset(pl(1), LAM / 6.0)
+            y2 = hlp.tile([P, PL], F32, name="y2")
+            t2 = hlp.tile([P, PL], F32, name="t2")
+            sg = hlp.tile([P, PL], F32, name="sg")
+            sn = hlp.tile([P, PL], F32, name="sn")
+            vv = hlp.tile([P, PL], F32, name="vv")
+            sp = hlp.tile([P, PL], F32, name="sp")
+            nc.scalar.activation(out=sg[:], in_=xv, func=ACT.Sigmoid)
+            nc.scalar.activation(out=sn[:], in_=xv, func=ACT.Sigmoid, scale=-1.0)
+            nc.scalar.activation(out=pl(2), in_=xv, func=ACT.Copy, scale=LAM)
+            nc.scalar.activation(out=y2[:], in_=xv, func=ACT.Square, scale=math.sqrt(8.0))
+            nc.scalar.activation(
+                out=t2[:], in_=y2[:], func=ACT.Square, scale=math.sqrt(2.0) / 2.0, bias=-2.0 * math.sqrt(2.0)
+            )
+            nc.scalar.activation(
+                out=pl(5), in_=y2[:], func=ACT.Square, scale=math.sqrt(0.5) / 2.0, bias=-1.5 * math.sqrt(0.5)
+            )
+            nc.scalar.activation(out=t2[:], in_=t2[:], func=ACT.Identity, scale=1.0, bias=-4.0)
+            nc.scalar.activation(out=pl(3), in_=y2[:], func=ACT.Identity, scale=0.375 * LAM, bias=-0.75 * LAM)
+            nc.gpsimd.tensor_tensor(out=vv[:], in0=sn[:], in1=xv, op=ALU.mult)
+            nc.vector.scalar_tensor_tensor(out=sp[:], in0=vv[:], scalar=1.0, in1=sg[:], op0=ALU.add, op1=ALU.mult)
+            nc.vector.scalar_tensor_tensor(out=pl(4), in0=y2[:], scalar=4.0, in1=pl(2), op0=ALU.subtract, op1=ALU.mult)
+            nc.vector.scalar_tensor_tensor(out=pl(6), in0=t2[:], scalar=2.0, in1=pl(2), op0=ALU.add, op1=ALU.mult)
+            nc.gpsimd.tensor_tensor(out=pl(8), in0=t2[:], in1=pl(4), op=ALU.mult)
+            nc.gpsimd.tensor_tensor(out=pl(7), in0=t2[:], in1=pl(3), op=ALU.mult)
+            nc.vector.tensor_scalar(out=pl(7), in0=pl(7), scalar1=7.0 / 6.0, scalar2=1.75 * LAM, op0=ALU.mult, op1=ALU.add)
+            nc.vector.scalar_tensor_tensor(out=pl(9), in0=pl(5), scalar=0.625, in1=t2[:], op0=ALU.subtract, op1=ALU.mult)
+            nc.vector.tensor_scalar(out=pl(9), in0=pl(9), scalar1=2.25 * LAM, scalar2=-2.25 * LAM, op0=ALU.mult, op1=ALU.add)
+            return u, sp
+
+        def mx(codes, scales, col, g0):
+            ps = pmx.tile([P, 512], F32, name="ps")
+            nc.tensor.matmul_mx(
+                out=ps[:],
+                lhsT=codes[:, col : col + P].bitcast(E4),
+                lhsT_scale=scales[:, col : col + P],
+                rhs=gcodes[:, g0 : g0 + 512].bitcast(E5),
+                rhs_scale=gscales[:, g0 : g0 + 512],
+                start=True,
+                stop=True,
+            )
+            return ps
+
+        def a_term(it, u, sp):
+            p0 = u[:, 0, 0:PL].rearrange("p (b j) -> p b j", b=10)
+            spv = sp[:].rearrange("p (b j) -> p b j", b=10)
+            for st, j0, j1 in ((0, 0, 51), (448, 51, 96), (576, 96, 104)):
+                ps = mx(bcodes, bscales, it * P, st)
+                m0 = 10 * j0 - st
+                nc.vector.tensor_tensor(
+                    out=p0[:, :, j0:j1],
+                    in0=spv[:, :, j0:j1],
+                    in1=ps[:, m0 : m0 + 10 * (j1 - j0)].rearrange("p (j b) -> p b j", b=10),
+                    op=ALU.mult,
+                )
+
+        def products(c, u, wc, ws):
+            for wi, ns in enumerate(((1, 6, 2, 7), (3, 8, 4, 9))):
+                ps = mx(wc, ws, c * P, 1024 + 512 * wi)
+                for k in range(2):
+                    n = ns[2 * k]
+                    a = n * PL + seg_addr(n, c)
+                    dst = u[:, :, a : a + J]
+                    src = ps[:, 2 * J * k : 2 * J * k + 2 * J].rearrange("p (e j) -> p e j", e=2)
+                    kap = (0.6 if n == 1 else 0.4) / LAM
+                    nc.vector.scalar_tensor_tensor(
+                        out=dst, in0=dst, scalar=kap, in1=src, op0=ALU.mult, op1=ALU.mult
+                    )
+                a = seg_addr(5, c) + 52 * wi
+                d5 = u[:, 1, a : a + 52]
+                nc.vector.scalar_tensor_tensor(
+                    out=d5, in0=d5, scalar=0.625, in1=ps[:, 416:468], op0=ALU.subtract, op1=ALU.mult
+                )
+
+        def sums(u, ot, classes):
+            pa = pac.tile([P, 4, P], F32, name="pa")
+            for k, beta in enumerate(classes):
+                for n in range(10):
+                    a = (n % 5) * PL + J * beta
+                    nc.tensor.matmul(
+                        out=pa[:, k, :],
+                        lhsT=u[:, n // 5, a : a + P],
+                        rhs=ident_f[:],
+                        is_transpose=True,
+                        start=(n == 0),
+                        stop=(n == 9),
+                    )
+            b0 = classes[0]
+            m = len(classes)
+            nc.scalar.copy(out=ot[:, b0 : b0 + 2 * m - 1 : 2, :], in_=pa[:, 0:m, :])
+
+        def store(it, ot):
+            cols = slice(it * P, (it + 1) * P)
+            nc.sync.dma_start(out=out[0:960, cols].rearrange("(j r) i -> j r i", r=10), in_=ot[0:96])
+            nc.sync.dma_start(out=out[960:1020, cols].rearrange("(j r) i -> j r i", r=10), in_=ot[96:102])
+            nc.sync.dma_start(
+                out=out[1020:1024, cols].rearrange("(o r) i -> o r i", o=1), in_=ot[102:103, 0:4, :]
+            )
+
+        nxt_w = prep_w(0)
+        nxt_b = basis(0)
+        for it in range(4):
+            wc, ws = nxt_w
+            u, sp = nxt_b
+            ot = otp.tile([P, 10, P], F32, name="ot")
+            if it < 3:
+                nxt_w = prep_w(it + 1)
+            a_term(it, u, sp)
+            for c in (0, 2, 4, 6, 8):
+                products(c, u, wc, ws)
+            sums(u, ot, (0, 2, 4, 6))
+            sums(u, ot, (8,))
+            for c in (1, 3, 5, 7, 9):
+                products(c, u, wc, ws)
+            if it < 3:
+                nxt_b = basis(it + 1)
+            sums(u, ot, (1, 3, 5, 7))
+            sums(u, ot, (9,))
+            store(it, ot)

@@ -17,9 +17,12 @@ FLOPS = 2 * 1024 * 512 * 5632
 
 P = 128
 J = 104
-PL = 10 * J
+PL = 5 * J
 EP = 5 * PL + 32
 LAM = 0.375
+LOOK = 5
+CHUNKS = (0, 2, 4, 6, 8, 1, 3, 5, 7, 9)
+WINDOWS = ((1, 6, 2, 7), (3, 8, 4, 9))
 
 
 def theta(n):
@@ -33,8 +36,8 @@ def seg_start(n):
 def seg_addr(n, c):
     t = theta(n)
     if c >= t:
-        return J * (c - t)
-    return J * (c - t + 10) - 1
+        return J * ((c - t) // 2)
+    return J * ((c - t + 10) // 2) - 1
 
 
 def tile_kantlinear_kernel(tc, x, base_weight, cheby_weight, grad_out, out):
@@ -45,39 +48,29 @@ def tile_kantlinear_kernel(tc, x, base_weight, cheby_weight, grad_out, out):
         grpp = ctx.enter_context(tc.tile_pool(name="grpp", bufs=3))
         keep = ctx.enter_context(tc.tile_pool(name="keep", bufs=1))
         wqp = ctx.enter_context(tc.tile_pool(name="wqp", bufs=2))
-        upl = ctx.enter_context(tc.tile_pool(name="upl", bufs=2))
-        hlp = ctx.enter_context(tc.tile_pool(name="hlp", bufs=1))
-        otp = ctx.enter_context(tc.tile_pool(name="otp", bufs=2))
-        pmx = ctx.enter_context(tc.psum_pool(name="pmx", bufs=4))
-        ptr = ctx.enter_context(tc.psum_pool(name="ptr", bufs=2))
+        upl = ctx.enter_context(tc.tile_pool(name="upl", bufs=4))
+        hlp = ctx.enter_context(tc.tile_pool(name="hlp", bufs=2))
+        otp = ctx.enter_context(tc.tile_pool(name="otp", bufs=3))
+        pmx = ctx.enter_context(tc.psum_pool(name="pmx", bufs=6))
         pac = ctx.enter_context(tc.psum_pool(name="pac", bufs=2))
+        ctx.enter_context(tc.manual_schedule())
 
         ident_f = const.tile([P, P], F32, name="ident_f")
         make_identity(nc, ident_f[:])
         ident_b = const.tile([P, P], BF16, name="ident_b")
         make_identity(nc, ident_b[:])
 
-        gs = rawp.tile([P, 8, 512], BF16, name="gs", tag="raw")
-        nc.sync.dma_start(out=gs[:], in_=grad_out.rearrange("(t p) k -> p t k", p=P))
-        xs = rawp.tile([P, 10, 512], BF16, name="xs", tag="raw")
-        nc.gpsimd.memset(xs[96:128], 0.0)
-        nc.sync.dma_start(out=xs[0:96], in_=x[0:960, :].rearrange("(j r) i -> j r i", r=10))
-        nc.sync.dma_start(out=xs[96:102], in_=x[960:1020, :].rearrange("(j r) i -> j r i", r=10))
-        nc.sync.dma_start(out=xs[102:103, 0:4, :], in_=x[1020:1024, :].rearrange("(o r) i -> o r i", o=1))
-        braw = rawp.tile([P, 4, 512], BF16, name="braw", tag="raw")
-        nc.sync.dma_start(
-            out=braw[:].rearrange("p (u e) n -> p u e n", u=2),
-            in_=base_weight.rearrange("(u q e) n -> q u e n", u=2, e=2),
-        )
         w4 = cheby_weight.rearrange("o i k -> o (i k)").rearrange("(u q e) n -> q u e n", u=2, e=2)
 
         def load_w(it):
             raw = rawp.tile([P, 4, 1280], BF16, name="raw", tag="raw")
             for t in range(4):
-                nc.sync.dma_start(
-                    out=raw[:, t, :].rearrange("p (c f) -> p c f", c=10),
-                    in_=w4[:, t // 2, t % 2, :].rearrange("q (c f) -> q c f", c=10)[:, :, it * P : (it + 1) * P],
-                )
+                src = w4[:, t // 2, t % 2, :].rearrange("q (c f) -> q c f", c=10)
+                dst = raw[:, t, :].rearrange("p (c f) -> p c f", c=10)
+                for par in range(2):
+                    nc.sync.dma_start(
+                        out=dst[:, 5 * par : 5 * par + 5, :], in_=src[:, par:10:2, it * P : (it + 1) * P]
+                    )
             return raw
 
         def regroup(dst, src, c0, c1, eng):
@@ -88,21 +81,44 @@ def tile_kantlinear_kernel(tc, x, base_weight, cheby_weight, grad_out, out):
             else:
                 nc.scalar.copy(out=d, in_=s)
 
+        def quant(codes, scales, grp, c0, c1, fmt):
+            nc.vector.quantize_mx(
+                out=codes[:, c0:c1].bitcast(fmt),
+                scales=scales[:, c0:c1],
+                in_=grp[:, c0:c1, :].rearrange("p r t -> p (r t)"),
+            )
+
+        gs = rawp.tile([P, 8, 512], BF16, name="gs", tag="raw")
+        nc.sync.dma_start(out=gs[:], in_=grad_out.rearrange("(t p) k -> p t k", p=P))
+        xs = rawp.tile([P, 10, 512], BF16, name="xs", tag="raw")
+        nc.gpsimd.memset(xs[96:128], 0.0)
+        nc.sync.dma_start(out=xs[0:96], in_=x[0:960, :].rearrange("(j r) i -> j r i", r=10))
+        nc.sync.dma_start(out=xs[96:102], in_=x[960:1020, :].rearrange("(j r) i -> j r i", r=10))
+        nc.sync.dma_start(out=xs[102:103, 0:4, :], in_=x[1020:1024, :].rearrange("(o r) i -> o r i", o=1))
+        raws = [load_w(0)]
+
         gn = grpp.tile([P, 1032, 4], BF16, name="gn", tag="grp", align_bytes=64)
         gn32 = gn[:].bitcast(F32)
         gs32 = gs[:].bitcast(F32)
         nc.vector.memset(gn32[:, 1024:1032, :], 0.0)
         for q in range(4):
-            pt = ptr.tile([P, 2, 256], F32, name="ptg", tag="tr")
+            pt = pmx.tile([P, 2, 256], F32, name="ptg", tag="ps")
             for b in range(2):
                 for u in range(2):
                     nc.tensor.transpose(
                         pt[:, u, b * P : (b + 1) * P], gs32[:, 2 * q + b, u * P : (u + 1) * P], ident_f[:]
                     )
-            nc.scalar.copy(out=gn32[:, 256 * q : 256 * q + 256, :], in_=pt[:].rearrange("p u r -> p r u"))
+            nc.vector.tensor_copy(out=gn32[:, 256 * q : 256 * q + 256, :], in_=pt[:].rearrange("p u r -> p r u"))
+        braw = rawp.tile([P, 4, 512], BF16, name="braw", tag="raw")
+        nc.sync.dma_start(
+            out=braw[:].rearrange("p (u e) n -> p u e n", u=2),
+            in_=base_weight.rearrange("(u q e) n -> q u e n", u=2, e=2),
+        )
+        ge = grpp.tile([P, 1024, 4], BF16, name="ge", tag="grp", align_bytes=64)
+        ge32 = ge[:].bitcast(F32)
         gw = grpp.tile([P, 1024, 4], BF16, name="gw", tag="grp", align_bytes=64)
         gw32 = gw[:].bitcast(F32)
-        for wi, ns in enumerate(((1, 6, 2, 7), (3, 8, 4, 9))):
+        for wi, ns in enumerate(WINDOWS):
             for k, n in enumerate(ns):
                 s = seg_start(n)
                 nc.vector.tensor_copy(
@@ -115,92 +131,142 @@ def tile_kantlinear_kernel(tc, x, base_weight, cheby_weight, grad_out, out):
         gcodes = keep.tile([P, 2048], U32, name="gcodes", align_bytes=64)
         gscales = keep.tile([P, 2048], U8, name="gscales", align_bytes=64)
         nc.vector.quantize_mx(
-            out=gcodes[:, 0:1024].bitcast(E5),
-            scales=gscales[:, 0:1024],
-            in_=gn[:, 0:1024, :].rearrange("p r t -> p (r t)"),
-        )
-        nc.vector.quantize_mx(
             out=gcodes[:, 1024:2048].bitcast(E5),
             scales=gscales[:, 1024:2048],
             in_=gw[:].rearrange("p r t -> p (r t)"),
         )
+        for par in range(2):
+            nc.vector.tensor_copy(out=ge32[:, 512 * par : 512 * par + 512, :], in_=gn32[:, par:1024:2, :])
+        nc.vector.quantize_mx(
+            out=gcodes[:, 0:1024].bitcast(E5),
+            scales=gscales[:, 0:1024],
+            in_=ge[:].rearrange("p r t -> p (r t)"),
+        )
 
         xT = keep.tile([P, 40, J], BF16, name="xT")
         for grp in range(5):
-            pt = ptr.tile([P, 8, P], BF16, name="ptx", tag="tr")
+            pt = pmx.tile([P, 8, P], BF16, name="ptx", tag="ps")
             for k in range(8):
-                it, beta = divmod(8 * grp + k, 10)
-                nc.tensor.transpose(pt[:, k, :], xs[:, beta, it * P : (it + 1) * P], ident_b[:])
+                h, bp = divmod(8 * grp + k, 5)
+                nc.tensor.transpose(
+                    pt[:, k, :], xs[:, 2 * bp + h % 2, (h // 2) * P : (h // 2 + 1) * P], ident_b[:]
+                )
             nc.scalar.copy(out=xT[:, 8 * grp : 8 * grp + 8, :], in_=pt[:, :, 0:J])
+        raws.append(load_w(1))
 
-        bgrp = grpp.tile([P, 512, 4], BF16, name="bgrp", tag="grp", align_bytes=64)
-        regroup(bgrp, braw, 0, 512, "v")
-        bcodes = keep.tile([P, 512], U32, name="bcodes", align_bytes=64)
-        bscales = keep.tile([P, 512], U8, name="bscales", align_bytes=64)
-        nc.vector.quantize_mx(
-            out=bcodes[:].bitcast(E4), scales=bscales[:], in_=bgrp[:].rearrange("p r t -> p (r t)")
-        )
+        state = {}
 
-        def prep_w(it):
-            raw = load_w(it)
-            grp = grpp.tile([P, 1280, 4], BF16, name="grp", tag="grp", align_bytes=64)
-            regroup(grp, raw, 0, 512, "v")
-            regroup(grp, raw, 512, 1024, "s")
-            regroup(grp, raw, 1024, 1280, "s")
-            wc = wqp.tile([P, 1280], U32, name="wc", align_bytes=64)
-            ws = wqp.tile([P, 1280], U8, name="ws", align_bytes=64)
-            nc.vector.quantize_mx(
-                out=wc[:, 0:1024].bitcast(E4),
-                scales=ws[:, 0:1024],
-                in_=grp[:, 0:1024, :].rearrange("p r t -> p (r t)"),
-            )
-            nc.vector.quantize_mx(
-                out=wc[:, 1024:1280].bitcast(E4),
-                scales=ws[:, 1024:1280],
-                in_=grp[:, 1024:1280, :].rearrange("p r t -> p (r t)"),
-            )
-            return wc, ws
+        def pl(u, n):
+            return u[:, n // 5, (n % 5) * PL : (n % 5) * PL + PL]
 
-        def basis(it):
+        def stage_sa(t):
             u = upl.tile([P, 2, EP], F32, name="u")
-
-            def pl(n):
-                return u[:, n // 5, (n % 5) * PL : (n % 5) * PL + PL]
-
-            xv = xT[:, 10 * it : 10 * it + 10, :].rearrange("p b j -> p (b j)")
-            nc.gpsimd.memset(u[:, :, 5 * PL : EP], 0.0)
-            nc.gpsimd.memset(pl(1), LAM / 6.0)
+            xv = xT[:, 5 * t : 5 * t + 5, :].rearrange("p b j -> p (b j)")
             y2 = hlp.tile([P, PL], F32, name="y2")
             t2 = hlp.tile([P, PL], F32, name="t2")
             sg = hlp.tile([P, PL], F32, name="sg")
             sn = hlp.tile([P, PL], F32, name="sn")
-            vv = hlp.tile([P, PL], F32, name="vv")
-            sp = hlp.tile([P, PL], F32, name="sp")
-            nc.scalar.activation(out=sg[:], in_=xv, func=ACT.Sigmoid)
-            nc.scalar.activation(out=sn[:], in_=xv, func=ACT.Sigmoid, scale=-1.0)
-            nc.scalar.activation(out=pl(2), in_=xv, func=ACT.Copy, scale=LAM)
+            state[t] = {"u": u, "xv": xv, "y2": y2, "t2": t2, "sg": sg, "sn": sn}
+            nc.gpsimd.memset(u[:, :, 5 * PL : EP], 0.0)
+            nc.gpsimd.memset(pl(u, 0), 0.0)
+            nc.gpsimd.memset(pl(u, 1), LAM / 6.0)
             nc.scalar.activation(out=y2[:], in_=xv, func=ACT.Square, scale=math.sqrt(8.0))
             nc.scalar.activation(
                 out=t2[:], in_=y2[:], func=ACT.Square, scale=math.sqrt(2.0) / 2.0, bias=-2.0 * math.sqrt(2.0)
             )
+            nc.scalar.activation(out=sn[:], in_=xv, func=ACT.Sigmoid, scale=-1.0)
+            nc.scalar.activation(out=pl(u, 2), in_=xv, func=ACT.Copy, scale=LAM)
             nc.scalar.activation(
-                out=pl(5), in_=y2[:], func=ACT.Square, scale=math.sqrt(0.5) / 2.0, bias=-1.5 * math.sqrt(0.5)
+                out=pl(u, 5), in_=y2[:], func=ACT.Square, scale=math.sqrt(0.5) / 2.0, bias=-1.5 * math.sqrt(0.5)
             )
-            nc.scalar.activation(out=t2[:], in_=t2[:], func=ACT.Identity, scale=1.0, bias=-4.0)
-            nc.scalar.activation(out=pl(3), in_=y2[:], func=ACT.Identity, scale=0.375 * LAM, bias=-0.75 * LAM)
-            nc.gpsimd.tensor_tensor(out=vv[:], in0=sn[:], in1=xv, op=ALU.mult)
-            nc.vector.scalar_tensor_tensor(out=sp[:], in0=vv[:], scalar=1.0, in1=sg[:], op0=ALU.add, op1=ALU.mult)
-            nc.vector.scalar_tensor_tensor(out=pl(4), in0=y2[:], scalar=4.0, in1=pl(2), op0=ALU.subtract, op1=ALU.mult)
-            nc.vector.scalar_tensor_tensor(out=pl(6), in0=t2[:], scalar=2.0, in1=pl(2), op0=ALU.add, op1=ALU.mult)
-            nc.gpsimd.tensor_tensor(out=pl(8), in0=t2[:], in1=pl(4), op=ALU.mult)
-            nc.gpsimd.tensor_tensor(out=pl(7), in0=t2[:], in1=pl(3), op=ALU.mult)
-            nc.vector.tensor_scalar(out=pl(7), in0=pl(7), scalar1=7.0 / 6.0, scalar2=1.75 * LAM, op0=ALU.mult, op1=ALU.add)
-            nc.vector.scalar_tensor_tensor(out=pl(9), in0=pl(5), scalar=0.625, in1=t2[:], op0=ALU.subtract, op1=ALU.mult)
-            nc.vector.tensor_scalar(out=pl(9), in0=pl(9), scalar1=2.25 * LAM, scalar2=-2.25 * LAM, op0=ALU.mult, op1=ALU.add)
-            return u, sp
+            nc.scalar.activation(out=sg[:], in_=xv, func=ACT.Sigmoid)
 
-        def mx(codes, scales, col, g0):
-            ps = pmx.tile([P, 512], F32, name="ps")
+        def stage_ga(t):
+            s = state[t]
+            u = s["u"]
+            vv = hlp.tile([P, PL], F32, name="vv")
+            s["vv"] = vv
+            nc.gpsimd.tensor_scalar(out=s["t2"][:], in0=s["t2"][:], scalar1=1.0, scalar2=-4.0, op0=ALU.mult, op1=ALU.add)
+            nc.gpsimd.tensor_scalar(
+                out=pl(u, 3), in0=s["y2"][:], scalar1=0.375 * LAM, scalar2=-0.75 * LAM, op0=ALU.mult, op1=ALU.add
+            )
+            nc.gpsimd.tensor_tensor(out=vv[:], in0=s["sn"][:], in1=s["xv"], op=ALU.mult)
+            nc.gpsimd.tensor_tensor(out=pl(u, 7), in0=s["t2"][:], in1=pl(u, 3), op=ALU.mult)
+            nc.gpsimd.tensor_scalar(
+                out=pl(u, 7), in0=pl(u, 7), scalar1=7.0 / 6.0, scalar2=1.75 * LAM, op0=ALU.mult, op1=ALU.add
+            )
+
+        def stage_va(t, part):
+            s = state[t]
+            u = s["u"]
+            if part == 0:
+                nc.vector.scalar_tensor_tensor(
+                    out=pl(u, 4), in0=s["y2"][:], scalar=4.0, in1=pl(u, 2), op0=ALU.subtract, op1=ALU.mult
+                )
+            elif part == 1:
+                nc.vector.scalar_tensor_tensor(
+                    out=pl(u, 9), in0=pl(u, 5), scalar=0.625, in1=s["t2"][:], op0=ALU.subtract, op1=ALU.mult
+                )
+            elif part == 2:
+                nc.vector.scalar_tensor_tensor(
+                    out=pl(u, 6), in0=s["t2"][:], scalar=2.0, in1=pl(u, 2), op0=ALU.add, op1=ALU.mult
+                )
+            else:
+                sp = hlp.tile([P, PL], F32, name="sp")
+                s["sp"] = sp
+                nc.vector.scalar_tensor_tensor(
+                    out=sp[:], in0=s["vv"][:], scalar=1.0, in1=s["sg"][:], op0=ALU.add, op1=ALU.mult
+                )
+
+        def stage_gb(t):
+            s = state[t]
+            u = s["u"]
+            nc.gpsimd.tensor_tensor(out=pl(u, 8), in0=s["t2"][:], in1=pl(u, 4), op=ALU.mult)
+            nc.gpsimd.tensor_scalar(
+                out=pl(u, 9), in0=pl(u, 9), scalar1=2.25 * LAM, scalar2=-2.25 * LAM, op0=ALU.mult, op1=ALU.add
+            )
+
+        stage_sa(0)
+        stage_ga(0)
+        wcs = {}
+
+        def new_w(it):
+            grp = grpp.tile([P, 1280, 4], BF16, name="grp", tag="grp", align_bytes=64)
+            wc = wqp.tile([P, 1280], U32, name="wc", align_bytes=64)
+            ws = wqp.tile([P, 1280], U8, name="ws", align_bytes=64)
+            wcs[it] = (wc, ws, grp)
+
+        new_w(0)
+        regroup(wcs[0][2], raws[0], 0, 512, "v")
+        regroup(wcs[0][2], raws[0], 512, 1280, "s")
+        quant(wcs[0][0], wcs[0][1], wcs[0][2], 0, 512, E4)
+        for part in range(3):
+            stage_va(0, part)
+        stage_gb(0)
+        quant(wcs[0][0], wcs[0][1], wcs[0][2], 512, 1024, E4)
+        quant(wcs[0][0], wcs[0][1], wcs[0][2], 1024, 1280, E4)
+        stage_va(0, 3)
+        raws.append(load_w(2))
+        stage_sa(1)
+        stage_ga(1)
+        bgrp = grpp.tile([P, 512, 4], BF16, name="bgrp", tag="grp", align_bytes=64)
+        regroup(bgrp, braw, 0, 512, "s")
+        bcodes = keep.tile([P, 512], U32, name="bcodes", align_bytes=64)
+        bscales = keep.tile([P, 512], U8, name="bscales", align_bytes=64)
+        raws.append(load_w(3))
+
+        jobs = [(h, j) for h in range(8) for j in range(11)]
+        banks = {}
+
+        def emit_mx(h, j):
+            ps = pmx.tile([P, 512], F32, name="ps", tag="ps")
+            banks[(h, j)] = ps
+            it, par = divmod(h, 2)
+            if j == 10:
+                codes, scales, col, g0 = bcodes, bscales, it * P, 512 * par
+            else:
+                codes, scales = wcs[it][0], wcs[it][1]
+                col, g0 = (5 * par + j // 2) * P, 1024 + 512 * (j % 2)
             nc.tensor.matmul_mx(
                 out=ps[:],
                 lhsT=codes[:, col : col + P].bitcast(E4),
@@ -210,81 +276,107 @@ def tile_kantlinear_kernel(tc, x, base_weight, cheby_weight, grad_out, out):
                 start=True,
                 stop=True,
             )
-            return ps
 
-        def a_term(it, u, sp):
-            p0 = u[:, 0, 0:PL].rearrange("p (b j) -> p b j", b=10)
-            spv = sp[:].rearrange("p (b j) -> p b j", b=10)
-            for st, j0, j1 in ((0, 0, 51), (448, 51, 96), (576, 96, 104)):
-                ps = mx(bcodes, bscales, it * P, st)
-                m0 = 10 * j0 - st
+        def consume(h, j):
+            ps = banks[(h, j)]
+            u = state[h]["u"]
+            if j == 10:
+                p0 = pl(u, 0).rearrange("p (b j) -> p b j", b=5)
+                spv = state[h]["sp"][:].rearrange("p (b j) -> p b j", b=5)
                 nc.vector.tensor_tensor(
-                    out=p0[:, :, j0:j1],
-                    in0=spv[:, :, j0:j1],
-                    in1=ps[:, m0 : m0 + 10 * (j1 - j0)].rearrange("p (j b) -> p b j", b=10),
+                    out=p0[:, :, 0:102],
+                    in0=spv[:, :, 0:102],
+                    in1=ps[:, 0:510].rearrange("p (j b) -> p b j", b=5),
                     op=ALU.mult,
                 )
-
-        def products(c, u, wc, ws):
-            for wi, ns in enumerate(((1, 6, 2, 7), (3, 8, 4, 9))):
-                ps = mx(wc, ws, c * P, 1024 + 512 * wi)
-                for k in range(2):
-                    n = ns[2 * k]
-                    a = n * PL + seg_addr(n, c)
-                    dst = u[:, :, a : a + J]
-                    src = ps[:, 2 * J * k : 2 * J * k + 2 * J].rearrange("p (e j) -> p e j", e=2)
-                    kap = (0.6 if n == 1 else 0.4) / LAM
-                    nc.vector.scalar_tensor_tensor(
-                        out=dst, in0=dst, scalar=kap, in1=src, op0=ALU.mult, op1=ALU.mult
-                    )
-                a = seg_addr(5, c) + 52 * wi
-                d5 = u[:, 1, a : a + 52]
-                nc.vector.scalar_tensor_tensor(
-                    out=d5, in0=d5, scalar=0.625, in1=ps[:, 416:468], op0=ALU.subtract, op1=ALU.mult
+                nc.vector.tensor_tensor(
+                    out=p0[:, 0:2, 102:103],
+                    in0=spv[:, 0:2, 102:103],
+                    in1=ps[:, 510:512].rearrange("p (j b) -> p b j", b=2),
+                    op=ALU.mult,
                 )
-
-        def sums(u, ot, classes):
-            pa = pac.tile([P, 4, P], F32, name="pa")
-            for k, beta in enumerate(classes):
-                for n in range(10):
-                    a = (n % 5) * PL + J * beta
-                    nc.tensor.matmul(
-                        out=pa[:, k, :],
-                        lhsT=u[:, n // 5, a : a + P],
-                        rhs=ident_f[:],
-                        is_transpose=True,
-                        start=(n == 0),
-                        stop=(n == 9),
-                    )
-            b0 = classes[0]
-            m = len(classes)
-            nc.scalar.copy(out=ot[:, b0 : b0 + 2 * m - 1 : 2, :], in_=pa[:, 0:m, :])
-
-        def store(it, ot):
-            cols = slice(it * P, (it + 1) * P)
-            nc.sync.dma_start(out=out[0:960, cols].rearrange("(j r) i -> j r i", r=10), in_=ot[0:96])
-            nc.sync.dma_start(out=out[960:1020, cols].rearrange("(j r) i -> j r i", r=10), in_=ot[96:102])
-            nc.sync.dma_start(
-                out=out[1020:1024, cols].rearrange("(o r) i -> o r i", o=1), in_=ot[102:103, 0:4, :]
+                return
+            c = 2 * (j // 2) + h % 2
+            wi = j % 2
+            for k in range(2):
+                n = WINDOWS[wi][2 * k]
+                a = n * PL + seg_addr(n, c)
+                dst = u[:, :, a : a + J]
+                src = ps[:, 2 * J * k : 2 * J * k + 2 * J].rearrange("p (e j) -> p e j", e=2)
+                kap = (0.6 if n == 1 else 0.4) / LAM
+                nc.vector.scalar_tensor_tensor(out=dst, in0=dst, scalar=kap, in1=src, op0=ALU.mult, op1=ALU.mult)
+            a = seg_addr(5, c) + 52 * wi
+            d5 = u[:, 1, a : a + 52]
+            nc.vector.scalar_tensor_tensor(
+                out=d5, in0=d5, scalar=0.625, in1=ps[:, 416:468], op0=ALU.subtract, op1=ALU.mult
             )
 
-        nxt_w = prep_w(0)
-        nxt_b = basis(0)
-        for it in range(4):
-            wc, ws = nxt_w
-            u, sp = nxt_b
-            ot = otp.tile([P, 10, P], F32, name="ot")
+        acc = {}
+
+        def bunch(h, bp):
+            u = state[h]["u"]
+            if bp == 0 or bp == 3:
+                acc[h] = pac.tile([P, 4, P], F32, name="pa")
+            if bp == 0:
+                state[h]["ot"] = otp.tile([P, 5, P], F32, name="ot")
+            pa = acc[h]
+            for n in range(10):
+                a = (n % 5) * PL + J * bp
+                nc.tensor.matmul(
+                    out=pa[:, bp % 3, :],
+                    lhsT=u[:, n // 5, a : a + P],
+                    rhs=ident_f[:],
+                    is_transpose=True,
+                    start=(n == 0),
+                    stop=(n == 9),
+                )
+            ot = state[h]["ot"]
+            if bp == 2:
+                nc.scalar.copy(out=ot[:, 0:3, :], in_=pa[:, 0:3, :])
+            if bp == 4:
+                nc.scalar.copy(out=ot[:, 3:5, :], in_=pa[:, 0:2, :])
+                it, par = divmod(h, 2)
+                cols = slice(it * P, (it + 1) * P)
+                nc.sync.dma_start(
+                    out=out[0:960, cols].rearrange("(j r) i -> j r i", r=10)[:, par:10:2, :], in_=ot[0:96]
+                )
+                nc.sync.dma_start(
+                    out=out[960:1020, cols].rearrange("(j r) i -> j r i", r=10)[:, par:10:2, :], in_=ot[96:102]
+                )
+                nc.sync.dma_start(
+                    out=out[1020:1024, cols].rearrange("(o r) i -> o r i", o=1)[:, par:4:2, :],
+                    in_=ot[102:103, 0:2, :],
+                )
+
+        for q in range(-LOOK, len(jobs)):
+            if q == -LOOK:
+                quant(bcodes, bscales, bgrp, 0, 512, E4)
+            if q + LOOK < len(jobs):
+                emit_mx(*jobs[q + LOOK])
+            if q < 0:
+                continue
+            h, j = jobs[q]
+            consume(h, j)
+            it, par = divmod(h, 2)
+            if j == 0 and h + 2 < 8:
+                stage_sa(h + 2)
+            if h + 1 < 8:
+                if j in (1, 3, 5, 7):
+                    stage_va(h + 1, (j - 1) // 2)
+                if j == 4:
+                    stage_gb(h + 1)
+            if j == 6 and h + 2 < 8:
+                stage_ga(h + 2)
             if it < 3:
-                nxt_w = prep_w(it + 1)
-            a_term(it, u, sp)
-            for c in (0, 2, 4, 6, 8):
-                products(c, u, wc, ws)
-            sums(u, ot, (0, 2, 4, 6))
-            sums(u, ot, (8,))
-            for c in (1, 3, 5, 7, 9):
-                products(c, u, wc, ws)
-            if it < 3:
-                nxt_b = basis(it + 1)
-            sums(u, ot, (1, 3, 5, 7))
-            sums(u, ot, (9,))
-            store(it, ot)
+                if par == 0 and j == 2:
+                    new_w(it + 1)
+                    regroup(wcs[it + 1][2], raws[it + 1], 0, 640, "s")
+                if par == 0 and j == 7:
+                    regroup(wcs[it + 1][2], raws[it + 1], 640, 1280, "s")
+                if par == 1 and j in (0, 2, 4):
+                    c0, c1 = ((0, 512), (512, 1024), (1024, 1280))[j // 2]
+                    quant(wcs[it + 1][0], wcs[it + 1][1], wcs[it + 1][2], c0, c1, E4)
+            if h > 0 and j in (1, 3, 5, 7, 9):
+                bunch(h - 1, (j - 1) // 2)
+        for bp in range(5):
+            bunch(7, bp)

@@ -165,8 +165,7 @@ def tile_kantlinear_kernel(tc, x, base_weight, cheby_weight, grad_out, out):
             y2 = hlp.tile([P, PL], F32, name="y2")
             t2 = hlp.tile([P, PL], F32, name="t2")
             sg = hlp.tile([P, PL], F32, name="sg")
-            sn = hlp.tile([P, PL], F32, name="sn")
-            state[t] = {"u": u, "xv": xv, "y2": y2, "t2": t2, "sg": sg, "sn": sn}
+            state[t] = {"u": u, "xv": xv, "y2": y2, "t2": t2, "sg": sg}
             nc.gpsimd.memset(u[:, :, 5 * PL : EP], 0.0)
             nc.gpsimd.memset(pl(u, 0), 0.0)
             nc.gpsimd.memset(pl(u, 1), LAM / 6.0)
@@ -174,60 +173,45 @@ def tile_kantlinear_kernel(tc, x, base_weight, cheby_weight, grad_out, out):
             nc.scalar.activation(
                 out=t2[:], in_=y2[:], func=ACT.Square, scale=math.sqrt(2.0) / 2.0, bias=-2.0 * math.sqrt(2.0)
             )
-            nc.scalar.activation(out=sn[:], in_=xv, func=ACT.Sigmoid, scale=-1.0)
-            nc.scalar.activation(out=pl(u, 2), in_=xv, func=ACT.Copy, scale=LAM)
+            nc.scalar.activation(out=pl(u, 3), in_=y2[:], func=ACT.Identity, scale=0.375 * LAM, bias=-0.75 * LAM)
             nc.scalar.activation(
                 out=pl(u, 5), in_=y2[:], func=ACT.Square, scale=math.sqrt(0.5) / 2.0, bias=-1.5 * math.sqrt(0.5)
             )
+            nc.scalar.activation(out=pl(u, 5), in_=pl(u, 5), func=ACT.Identity, scale=1.0, bias=-0.625)
+            nc.scalar.activation(out=pl(u, 2), in_=xv, func=ACT.Copy, scale=LAM)
             nc.scalar.activation(out=sg[:], in_=xv, func=ACT.Sigmoid)
 
-        def stage_ga(t):
-            s = state[t]
-            u = s["u"]
-            vv = hlp.tile([P, PL], F32, name="vv")
-            s["vv"] = vv
-            nc.gpsimd.tensor_scalar(out=s["t2"][:], in0=s["t2"][:], scalar1=1.0, scalar2=-4.0, op0=ALU.mult, op1=ALU.add)
-            nc.gpsimd.tensor_scalar(
-                out=pl(u, 3), in0=s["y2"][:], scalar1=0.375 * LAM, scalar2=-0.75 * LAM, op0=ALU.mult, op1=ALU.add
-            )
-            nc.gpsimd.tensor_tensor(out=vv[:], in0=s["sn"][:], in1=s["xv"], op=ALU.mult)
-            nc.gpsimd.tensor_tensor(out=pl(u, 7), in0=s["t2"][:], in1=pl(u, 3), op=ALU.mult)
-            nc.gpsimd.tensor_scalar(
-                out=pl(u, 7), in0=pl(u, 7), scalar1=7.0 / 6.0, scalar2=1.75 * LAM, op0=ALU.mult, op1=ALU.add
-            )
+        def stt(o, a, sc, b, op0):
+            nc.vector.scalar_tensor_tensor(out=o, in0=a, scalar=sc, in1=b, op0=op0, op1=ALU.mult)
 
         def stage_va(t, part):
             s = state[t]
             u = s["u"]
             if part == 0:
-                nc.vector.scalar_tensor_tensor(
-                    out=pl(u, 4), in0=s["y2"][:], scalar=4.0, in1=pl(u, 2), op0=ALU.subtract, op1=ALU.mult
-                )
+                stt(pl(u, 7), s["t2"][:], 4.0, pl(u, 3), ALU.subtract)
             elif part == 1:
-                nc.vector.scalar_tensor_tensor(
-                    out=pl(u, 9), in0=pl(u, 5), scalar=0.625, in1=s["t2"][:], op0=ALU.subtract, op1=ALU.mult
-                )
+                stt(pl(u, 9), s["t2"][:], 4.0, pl(u, 5), ALU.subtract)
             elif part == 2:
-                nc.vector.scalar_tensor_tensor(
-                    out=pl(u, 6), in0=s["t2"][:], scalar=2.0, in1=pl(u, 2), op0=ALU.add, op1=ALU.mult
-                )
+                stt(pl(u, 4), s["y2"][:], 4.0, pl(u, 2), ALU.subtract)
+            elif part == 3:
+                stt(pl(u, 8), s["t2"][:], 4.0, pl(u, 4), ALU.subtract)
+            elif part == 4:
+                stt(pl(u, 6), s["t2"][:], 2.0, pl(u, 2), ALU.subtract)
+            elif part == 5:
+                vv = hlp.tile([P, PL], F32, name="vv")
+                s["vv"] = vv
+                stt(vv[:], s["sg"][:], 1.0, s["xv"], ALU.subtract)
             else:
                 sp = hlp.tile([P, PL], F32, name="sp")
                 s["sp"] = sp
-                nc.vector.scalar_tensor_tensor(
-                    out=sp[:], in0=s["vv"][:], scalar=1.0, in1=s["sg"][:], op0=ALU.add, op1=ALU.mult
-                )
+                stt(sp[:], s["vv"][:], 1.0, s["sg"][:], ALU.subtract)
 
-        def stage_gb(t):
-            s = state[t]
-            u = s["u"]
-            nc.gpsimd.tensor_tensor(out=pl(u, 8), in0=s["t2"][:], in1=pl(u, 4), op=ALU.mult)
-            nc.gpsimd.tensor_scalar(
-                out=pl(u, 9), in0=pl(u, 9), scalar1=2.25 * LAM, scalar2=-2.25 * LAM, op0=ALU.mult, op1=ALU.add
-            )
+        def stage_sb(t):
+            u = state[t]["u"]
+            nc.scalar.activation(out=pl(u, 7), in_=pl(u, 7), func=ACT.Identity, scale=7.0 / 6.0, bias=1.75 * LAM)
+            nc.scalar.activation(out=pl(u, 9), in_=pl(u, 9), func=ACT.Identity, scale=2.25 * LAM, bias=-2.25 * LAM)
 
         stage_sa(0)
-        stage_ga(0)
         wcs = {}
 
         def new_w(it):
@@ -240,15 +224,15 @@ def tile_kantlinear_kernel(tc, x, base_weight, cheby_weight, grad_out, out):
         regroup(wcs[0][2], raws[0], 0, 512, "v")
         regroup(wcs[0][2], raws[0], 512, 1280, "s")
         quant(wcs[0][0], wcs[0][1], wcs[0][2], 0, 512, E4)
-        for part in range(3):
+        for part in range(5):
             stage_va(0, part)
-        stage_gb(0)
+        stage_sb(0)
         quant(wcs[0][0], wcs[0][1], wcs[0][2], 512, 1024, E4)
         quant(wcs[0][0], wcs[0][1], wcs[0][2], 1024, 1280, E4)
-        stage_va(0, 3)
+        stage_va(0, 5)
+        stage_va(0, 6)
         raws.append(load_w(2))
         stage_sa(1)
-        stage_ga(1)
         bgrp = grpp.tile([P, 512, 4], BF16, name="bgrp", tag="grp", align_bytes=64)
         regroup(bgrp, braw, 0, 512, "s")
         bcodes = keep.tile([P, 512], U32, name="bcodes", align_bytes=64)
@@ -283,17 +267,13 @@ def tile_kantlinear_kernel(tc, x, base_weight, cheby_weight, grad_out, out):
             if j == 10:
                 p0 = pl(u, 0).rearrange("p (b j) -> p b j", b=5)
                 spv = state[h]["sp"][:].rearrange("p (b j) -> p b j", b=5)
-                nc.vector.tensor_tensor(
-                    out=p0[:, :, 0:102],
-                    in0=spv[:, :, 0:102],
-                    in1=ps[:, 0:510].rearrange("p (j b) -> p b j", b=5),
-                    op=ALU.mult,
-                )
-                nc.vector.tensor_tensor(
-                    out=p0[:, 0:2, 102:103],
-                    in0=spv[:, 0:2, 102:103],
-                    in1=ps[:, 510:512].rearrange("p (j b) -> p b j", b=2),
-                    op=ALU.mult,
+                stt(p0[:, :, 0:102], spv[:, :, 0:102], -1.0, ps[:, 0:510].rearrange("p (j b) -> p b j", b=5), ALU.mult)
+                stt(
+                    p0[:, 0:2, 102:103],
+                    spv[:, 0:2, 102:103],
+                    -1.0,
+                    ps[:, 510:512].rearrange("p (j b) -> p b j", b=2),
+                    ALU.mult,
                 )
                 return
             c = 2 * (j // 2) + h % 2
@@ -307,9 +287,7 @@ def tile_kantlinear_kernel(tc, x, base_weight, cheby_weight, grad_out, out):
                 nc.vector.scalar_tensor_tensor(out=dst, in0=dst, scalar=kap, in1=src, op0=ALU.mult, op1=ALU.mult)
             a = seg_addr(5, c) + 52 * wi
             d5 = u[:, 1, a : a + 52]
-            nc.vector.scalar_tensor_tensor(
-                out=d5, in0=d5, scalar=0.625, in1=ps[:, 416:468], op0=ALU.subtract, op1=ALU.mult
-            )
+            nc.vector.tensor_tensor(out=d5, in0=d5, in1=ps[:, 416:468], op=ALU.mult)
 
         acc = {}
 
@@ -361,12 +339,10 @@ def tile_kantlinear_kernel(tc, x, base_weight, cheby_weight, grad_out, out):
             if j == 0 and h + 2 < 8:
                 stage_sa(h + 2)
             if h + 1 < 8:
-                if j in (1, 3, 5, 7):
-                    stage_va(h + 1, (j - 1) // 2)
-                if j == 4:
-                    stage_gb(h + 1)
-            if j == 6 and h + 2 < 8:
-                stage_ga(h + 2)
+                if j < 7:
+                    stage_va(h + 1, j)
+                if j == 3:
+                    stage_sb(h + 1)
             if it < 3:
                 if par == 0 and j == 2:
                     new_w(it + 1)

@@ -20,7 +20,7 @@ J = 104
 PL = 5 * J
 EP = 5 * PL + 32
 LAM = 0.375
-LOOK = 5
+LOOK = 4
 CHUNKS = (0, 2, 4, 6, 8, 1, 3, 5, 7, 9)
 WINDOWS = ((1, 6, 2, 7), (3, 8, 4, 9))
 
@@ -51,8 +51,8 @@ def tile_kantlinear_kernel(tc, x, base_weight, cheby_weight, grad_out, out):
         upl = ctx.enter_context(tc.tile_pool(name="upl", bufs=4))
         hlp = ctx.enter_context(tc.tile_pool(name="hlp", bufs=2))
         otp = ctx.enter_context(tc.tile_pool(name="otp", bufs=3))
-        pmx = ctx.enter_context(tc.psum_pool(name="pmx", bufs=6))
-        pac = ctx.enter_context(tc.psum_pool(name="pac", bufs=2))
+        pmx = ctx.enter_context(tc.psum_pool(name="pmx", bufs=5))
+        pac = ctx.enter_context(tc.psum_pool(name="pac", bufs=1))
         ctx.enter_context(tc.manual_schedule())
 
         ident_f = const.tile([P, P], F32, name="ident_f")
@@ -108,7 +108,7 @@ def tile_kantlinear_kernel(tc, x, base_weight, cheby_weight, grad_out, out):
                     nc.tensor.transpose(
                         pt[:, u, b * P : (b + 1) * P], gs32[:, 2 * q + b, u * P : (u + 1) * P], ident_f[:]
                     )
-            nc.vector.tensor_copy(out=gn32[:, 256 * q : 256 * q + 256, :], in_=pt[:].rearrange("p u r -> p r u"))
+            nc.scalar.copy(out=gn32[:, 256 * q : 256 * q + 256, :], in_=pt[:].rearrange("p u r -> p r u"))
         braw = rawp.tile([P, 4, 512], BF16, name="braw", tag="raw")
         nc.sync.dma_start(
             out=braw[:].rearrange("p (u e) n -> p u e n", u=2),
@@ -165,7 +165,8 @@ def tile_kantlinear_kernel(tc, x, base_weight, cheby_weight, grad_out, out):
             y2 = hlp.tile([P, PL], F32, name="y2")
             t2 = hlp.tile([P, PL], F32, name="t2")
             sg = hlp.tile([P, PL], F32, name="sg")
-            state[t] = {"u": u, "xv": xv, "y2": y2, "t2": t2, "sg": sg}
+            sn = hlp.tile([P, PL], F32, name="sn")
+            state[t] = {"u": u, "xv": xv, "y2": y2, "t2": t2, "sg": sg, "sn": sn}
             nc.gpsimd.memset(u[:, :, 5 * PL : EP], 0.0)
             nc.gpsimd.memset(pl(u, 0), 0.0)
             nc.gpsimd.memset(pl(u, 1), LAM / 6.0)
@@ -173,45 +174,60 @@ def tile_kantlinear_kernel(tc, x, base_weight, cheby_weight, grad_out, out):
             nc.scalar.activation(
                 out=t2[:], in_=y2[:], func=ACT.Square, scale=math.sqrt(2.0) / 2.0, bias=-2.0 * math.sqrt(2.0)
             )
-            nc.scalar.activation(out=pl(u, 3), in_=y2[:], func=ACT.Identity, scale=0.375 * LAM, bias=-0.75 * LAM)
+            nc.scalar.activation(out=sn[:], in_=xv, func=ACT.Sigmoid, scale=-1.0)
+            nc.scalar.activation(out=pl(u, 2), in_=xv, func=ACT.Copy, scale=LAM)
             nc.scalar.activation(
                 out=pl(u, 5), in_=y2[:], func=ACT.Square, scale=math.sqrt(0.5) / 2.0, bias=-1.5 * math.sqrt(0.5)
             )
-            nc.scalar.activation(out=pl(u, 5), in_=pl(u, 5), func=ACT.Identity, scale=1.0, bias=-0.625)
-            nc.scalar.activation(out=pl(u, 2), in_=xv, func=ACT.Copy, scale=LAM)
             nc.scalar.activation(out=sg[:], in_=xv, func=ACT.Sigmoid)
 
-        def stt(o, a, sc, b, op0):
-            nc.vector.scalar_tensor_tensor(out=o, in0=a, scalar=sc, in1=b, op0=op0, op1=ALU.mult)
+        def stage_ga(t):
+            s = state[t]
+            u = s["u"]
+            vv = hlp.tile([P, PL], F32, name="vv")
+            s["vv"] = vv
+            nc.gpsimd.tensor_scalar(out=s["t2"][:], in0=s["t2"][:], scalar1=1.0, scalar2=-4.0, op0=ALU.mult, op1=ALU.add)
+            nc.gpsimd.tensor_scalar(
+                out=pl(u, 3), in0=s["y2"][:], scalar1=0.375 * LAM, scalar2=-0.75 * LAM, op0=ALU.mult, op1=ALU.add
+            )
+            nc.gpsimd.tensor_tensor(out=vv[:], in0=s["sn"][:], in1=s["xv"], op=ALU.mult)
+            nc.gpsimd.tensor_tensor(out=pl(u, 7), in0=s["t2"][:], in1=pl(u, 3), op=ALU.mult)
+            nc.gpsimd.tensor_scalar(
+                out=pl(u, 7), in0=pl(u, 7), scalar1=7.0 / 6.0, scalar2=1.75 * LAM, op0=ALU.mult, op1=ALU.add
+            )
 
         def stage_va(t, part):
             s = state[t]
             u = s["u"]
             if part == 0:
-                stt(pl(u, 7), s["t2"][:], 4.0, pl(u, 3), ALU.subtract)
+                nc.vector.scalar_tensor_tensor(
+                    out=pl(u, 4), in0=s["y2"][:], scalar=4.0, in1=pl(u, 2), op0=ALU.subtract, op1=ALU.mult
+                )
             elif part == 1:
-                stt(pl(u, 9), s["t2"][:], 4.0, pl(u, 5), ALU.subtract)
+                nc.vector.scalar_tensor_tensor(
+                    out=pl(u, 9), in0=pl(u, 5), scalar=0.625, in1=s["t2"][:], op0=ALU.subtract, op1=ALU.mult
+                )
             elif part == 2:
-                stt(pl(u, 4), s["y2"][:], 4.0, pl(u, 2), ALU.subtract)
-            elif part == 3:
-                stt(pl(u, 8), s["t2"][:], 4.0, pl(u, 4), ALU.subtract)
-            elif part == 4:
-                stt(pl(u, 6), s["t2"][:], 2.0, pl(u, 2), ALU.subtract)
-            elif part == 5:
-                vv = hlp.tile([P, PL], F32, name="vv")
-                s["vv"] = vv
-                stt(vv[:], s["sg"][:], 1.0, s["xv"], ALU.subtract)
+                nc.vector.scalar_tensor_tensor(
+                    out=pl(u, 6), in0=s["t2"][:], scalar=2.0, in1=pl(u, 2), op0=ALU.add, op1=ALU.mult
+                )
             else:
                 sp = hlp.tile([P, PL], F32, name="sp")
                 s["sp"] = sp
-                stt(sp[:], s["vv"][:], 1.0, s["sg"][:], ALU.subtract)
+                nc.vector.scalar_tensor_tensor(
+                    out=sp[:], in0=s["vv"][:], scalar=1.0, in1=s["sg"][:], op0=ALU.add, op1=ALU.mult
+                )
 
-        def stage_sb(t):
-            u = state[t]["u"]
-            nc.scalar.activation(out=pl(u, 7), in_=pl(u, 7), func=ACT.Identity, scale=7.0 / 6.0, bias=1.75 * LAM)
-            nc.scalar.activation(out=pl(u, 9), in_=pl(u, 9), func=ACT.Identity, scale=2.25 * LAM, bias=-2.25 * LAM)
+        def stage_gb(t):
+            s = state[t]
+            u = s["u"]
+            nc.gpsimd.tensor_tensor(out=pl(u, 8), in0=s["t2"][:], in1=pl(u, 4), op=ALU.mult)
+            nc.gpsimd.tensor_scalar(
+                out=pl(u, 9), in0=pl(u, 9), scalar1=2.25 * LAM, scalar2=-2.25 * LAM, op0=ALU.mult, op1=ALU.add
+            )
 
         stage_sa(0)
+        stage_ga(0)
         wcs = {}
 
         def new_w(it):
@@ -224,15 +240,15 @@ def tile_kantlinear_kernel(tc, x, base_weight, cheby_weight, grad_out, out):
         regroup(wcs[0][2], raws[0], 0, 512, "v")
         regroup(wcs[0][2], raws[0], 512, 1280, "s")
         quant(wcs[0][0], wcs[0][1], wcs[0][2], 0, 512, E4)
-        for part in range(5):
+        for part in range(3):
             stage_va(0, part)
-        stage_sb(0)
+        stage_gb(0)
         quant(wcs[0][0], wcs[0][1], wcs[0][2], 512, 1024, E4)
         quant(wcs[0][0], wcs[0][1], wcs[0][2], 1024, 1280, E4)
-        stage_va(0, 5)
-        stage_va(0, 6)
+        stage_va(0, 3)
         raws.append(load_w(2))
         stage_sa(1)
+        stage_ga(1)
         bgrp = grpp.tile([P, 512, 4], BF16, name="bgrp", tag="grp", align_bytes=64)
         regroup(bgrp, braw, 0, 512, "s")
         bcodes = keep.tile([P, 512], U32, name="bcodes", align_bytes=64)
@@ -267,13 +283,17 @@ def tile_kantlinear_kernel(tc, x, base_weight, cheby_weight, grad_out, out):
             if j == 10:
                 p0 = pl(u, 0).rearrange("p (b j) -> p b j", b=5)
                 spv = state[h]["sp"][:].rearrange("p (b j) -> p b j", b=5)
-                stt(p0[:, :, 0:102], spv[:, :, 0:102], -1.0, ps[:, 0:510].rearrange("p (j b) -> p b j", b=5), ALU.mult)
-                stt(
-                    p0[:, 0:2, 102:103],
-                    spv[:, 0:2, 102:103],
-                    -1.0,
-                    ps[:, 510:512].rearrange("p (j b) -> p b j", b=2),
-                    ALU.mult,
+                nc.vector.tensor_tensor(
+                    out=p0[:, :, 0:102],
+                    in0=spv[:, :, 0:102],
+                    in1=ps[:, 0:510].rearrange("p (j b) -> p b j", b=5),
+                    op=ALU.mult,
+                )
+                nc.vector.tensor_tensor(
+                    out=p0[:, 0:2, 102:103],
+                    in0=spv[:, 0:2, 102:103],
+                    in1=ps[:, 510:512].rearrange("p (j b) -> p b j", b=2),
+                    op=ALU.mult,
                 )
                 return
             c = 2 * (j // 2) + h % 2
@@ -287,21 +307,24 @@ def tile_kantlinear_kernel(tc, x, base_weight, cheby_weight, grad_out, out):
                 nc.vector.scalar_tensor_tensor(out=dst, in0=dst, scalar=kap, in1=src, op0=ALU.mult, op1=ALU.mult)
             a = seg_addr(5, c) + 52 * wi
             d5 = u[:, 1, a : a + 52]
-            nc.vector.tensor_tensor(out=d5, in0=d5, in1=ps[:, 416:468], op=ALU.mult)
+            nc.vector.scalar_tensor_tensor(
+                out=d5, in0=d5, scalar=0.625, in1=ps[:, 416:468], op0=ALU.subtract, op1=ALU.mult
+            )
 
         acc = {}
+        order = [(n, b) for n in range(10) for b in (0, 1, 2)] + [(n, b) for n in range(10) for b in (3, 4)]
+        cuts = (0, 15, 30, 40, 50)
 
-        def bunch(h, bp):
+        def bunch(h, i):
             u = state[h]["u"]
-            if bp == 0 or bp == 3:
-                acc[h] = pac.tile([P, 4, P], F32, name="pa")
-            if bp == 0:
+            if i == 0:
+                acc[h] = [pac.tile([P, 2, P], F32, name="pa%d" % b) for b in range(3)]
                 state[h]["ot"] = otp.tile([P, 5, P], F32, name="ot")
-            pa = acc[h]
-            for n in range(10):
+            pas = acc[h]
+            for n, bp in order[cuts[i] : cuts[i + 1]]:
                 a = (n % 5) * PL + J * bp
                 nc.tensor.matmul(
-                    out=pa[:, bp % 3, :],
+                    out=pas[bp % 3][:, bp // 3, :],
                     lhsT=u[:, n // 5, a : a + P],
                     rhs=ident_f[:],
                     is_transpose=True,
@@ -309,10 +332,11 @@ def tile_kantlinear_kernel(tc, x, base_weight, cheby_weight, grad_out, out):
                     stop=(n == 9),
                 )
             ot = state[h]["ot"]
-            if bp == 2:
-                nc.scalar.copy(out=ot[:, 0:3, :], in_=pa[:, 0:3, :])
-            if bp == 4:
-                nc.scalar.copy(out=ot[:, 3:5, :], in_=pa[:, 0:2, :])
+            if i == 1:
+                nc.scalar.copy(out=ot[:, 2:3, :], in_=pas[2][:, 0:1, :])
+            if i == 3:
+                nc.scalar.copy(out=ot[:, 0:4:3, :], in_=pas[0][:])
+                nc.scalar.copy(out=ot[:, 1:5:3, :], in_=pas[1][:])
                 it, par = divmod(h, 2)
                 cols = slice(it * P, (it + 1) * P)
                 nc.sync.dma_start(
@@ -339,10 +363,12 @@ def tile_kantlinear_kernel(tc, x, base_weight, cheby_weight, grad_out, out):
             if j == 0 and h + 2 < 8:
                 stage_sa(h + 2)
             if h + 1 < 8:
-                if j < 7:
-                    stage_va(h + 1, j)
-                if j == 3:
-                    stage_sb(h + 1)
+                if j in (1, 3, 5, 7):
+                    stage_va(h + 1, (j - 1) // 2)
+                if j == 4:
+                    stage_gb(h + 1)
+            if j == 6 and h + 2 < 8:
+                stage_ga(h + 2)
             if it < 3:
                 if par == 0 and j == 2:
                     new_w(it + 1)
@@ -352,7 +378,7 @@ def tile_kantlinear_kernel(tc, x, base_weight, cheby_weight, grad_out, out):
                 if par == 1 and j in (0, 2, 4):
                     c0, c1 = ((0, 512), (512, 1024), (1024, 1280))[j // 2]
                     quant(wcs[it + 1][0], wcs[it + 1][1], wcs[it + 1][2], c0, c1, E4)
-            if h > 0 and j in (1, 3, 5, 7, 9):
+            if h > 0 and j in (1, 3, 5, 7):
                 bunch(h - 1, (j - 1) // 2)
-        for bp in range(5):
-            bunch(7, bp)
+        for i in range(4):
+            bunch(7, i)

@@ -21,7 +21,7 @@ PL = 5 * J
 EP = 5 * PL + 32
 LAM = 0.375
 LOOK = 4
-CHUNKS = (0, 2, 4, 6, 8, 1, 3, 5, 7, 9)
+NJ = 16
 WINDOWS = ((1, 6, 2, 7), (3, 8, 4, 9))
 
 
@@ -50,7 +50,7 @@ def tile_kantlinear_kernel(tc, x, base_weight, cheby_weight, grad_out, out):
         wqp = ctx.enter_context(tc.tile_pool(name="wqp", bufs=2))
         upl = ctx.enter_context(tc.tile_pool(name="upl", bufs=4))
         hlp = ctx.enter_context(tc.tile_pool(name="hlp", bufs=2))
-        otp = ctx.enter_context(tc.tile_pool(name="otp", bufs=3))
+        otp = ctx.enter_context(tc.tile_pool(name="otp", bufs=2))
         pmx = ctx.enter_context(tc.psum_pool(name="pmx", bufs=5))
         pac = ctx.enter_context(tc.psum_pool(name="pac", bufs=1))
         ctx.enter_context(tc.manual_schedule())
@@ -81,10 +81,10 @@ def tile_kantlinear_kernel(tc, x, base_weight, cheby_weight, grad_out, out):
             else:
                 nc.scalar.copy(out=d, in_=s)
 
-        def quant(codes, scales, grp, c0, c1, fmt):
+        def quant(codes, scales, grp, c0, c1, fmt, g0=0):
             nc.vector.quantize_mx(
-                out=codes[:, c0:c1].bitcast(fmt),
-                scales=scales[:, c0:c1],
+                out=codes[:, g0 + c0 : g0 + c1].bitcast(fmt),
+                scales=scales[:, g0 + c0 : g0 + c1],
                 in_=grp[:, c0:c1, :].rearrange("p r t -> p (r t)"),
             )
 
@@ -116,7 +116,7 @@ def tile_kantlinear_kernel(tc, x, base_weight, cheby_weight, grad_out, out):
         )
         ge = grpp.tile([P, 1024, 4], BF16, name="ge", tag="grp", align_bytes=64)
         ge32 = ge[:].bitcast(F32)
-        gw = grpp.tile([P, 1024, 4], BF16, name="gw", tag="grp", align_bytes=64)
+        gw = grpp.tile([P, 1536, 4], BF16, name="gw", tag="grp", align_bytes=64)
         gw32 = gw[:].bitcast(F32)
         for wi, ns in enumerate(WINDOWS):
             for k, n in enumerate(ns):
@@ -124,24 +124,15 @@ def tile_kantlinear_kernel(tc, x, base_weight, cheby_weight, grad_out, out):
                 nc.vector.tensor_copy(
                     out=gw32[:, 512 * wi + J * k : 512 * wi + J * k + J, :], in_=gn32[:, s : s + J, :]
                 )
-            nc.vector.tensor_copy(
-                out=gw32[:, 512 * wi + 416 : 512 * wi + 468, :], in_=gn32[:, 512 + 52 * wi : 564 + 52 * wi, :]
-            )
-            nc.vector.memset(gw32[:, 512 * wi + 468 : 512 * wi + 512, :], 0.0)
-        gcodes = keep.tile([P, 2048], U32, name="gcodes", align_bytes=64)
-        gscales = keep.tile([P, 2048], U8, name="gscales", align_bytes=64)
-        nc.vector.quantize_mx(
-            out=gcodes[:, 1024:2048].bitcast(E5),
-            scales=gscales[:, 1024:2048],
-            in_=gw[:].rearrange("p r t -> p (r t)"),
-        )
+            nc.vector.memset(gw32[:, 512 * wi + 416 : 512 * wi + 512, :], 0.0)
+        nc.vector.tensor_copy(out=gw32[:, 1024:1536, :], in_=gn32[:, 512:1024, :])
+        gcodes = keep.tile([P, 2560], U32, name="gcodes", align_bytes=64)
+        gscales = keep.tile([P, 2560], U8, name="gscales", align_bytes=64)
+        quant(gcodes, gscales, gw, 0, 1024, E5, 1024)
+        quant(gcodes, gscales, gw, 1024, 1536, E5, 1024)
         for par in range(2):
             nc.vector.tensor_copy(out=ge32[:, 512 * par : 512 * par + 512, :], in_=gn32[:, par:1024:2, :])
-        nc.vector.quantize_mx(
-            out=gcodes[:, 0:1024].bitcast(E5),
-            scales=gscales[:, 0:1024],
-            in_=ge[:].rearrange("p r t -> p (r t)"),
-        )
+        quant(gcodes, gscales, ge, 0, 1024, E5)
 
         xT = keep.tile([P, 40, J], BF16, name="xT")
         for grp in range(5):
@@ -166,68 +157,52 @@ def tile_kantlinear_kernel(tc, x, base_weight, cheby_weight, grad_out, out):
             t2 = hlp.tile([P, PL], F32, name="t2")
             sg = hlp.tile([P, PL], F32, name="sg")
             sn = hlp.tile([P, PL], F32, name="sn")
-            state[t] = {"u": u, "xv": xv, "y2": y2, "t2": t2, "sg": sg, "sn": sn}
+            vv = hlp.tile([P, PL], F32, name="vv")
+            state[t] = {"u": u, "xv": xv, "y2": y2, "t2": t2, "sg": sg, "sn": sn, "vv": vv}
             nc.gpsimd.memset(u[:, :, 5 * PL : EP], 0.0)
             nc.gpsimd.memset(pl(u, 0), 0.0)
             nc.gpsimd.memset(pl(u, 1), LAM / 6.0)
+            nc.scalar.activation(out=sn[:], in_=xv, func=ACT.Sigmoid, scale=-1.0)
+            nc.gpsimd.tensor_tensor(out=vv[:], in0=sn[:], in1=xv, op=ALU.mult)
             nc.scalar.activation(out=y2[:], in_=xv, func=ACT.Square, scale=math.sqrt(8.0))
             nc.scalar.activation(
                 out=t2[:], in_=y2[:], func=ACT.Square, scale=math.sqrt(2.0) / 2.0, bias=-2.0 * math.sqrt(2.0)
             )
-            nc.scalar.activation(out=sn[:], in_=xv, func=ACT.Sigmoid, scale=-1.0)
-            nc.scalar.activation(out=pl(u, 2), in_=xv, func=ACT.Copy, scale=LAM)
+            nc.scalar.activation(out=pl(u, 3), in_=y2[:], func=ACT.Identity, scale=0.375 * LAM, bias=-0.75 * LAM)
             nc.scalar.activation(
                 out=pl(u, 5), in_=y2[:], func=ACT.Square, scale=math.sqrt(0.5) / 2.0, bias=-1.5 * math.sqrt(0.5)
             )
+            nc.scalar.activation(out=pl(u, 5), in_=pl(u, 5), func=ACT.Identity, scale=1.0, bias=-0.625)
+            nc.scalar.activation(out=pl(u, 2), in_=xv, func=ACT.Copy, scale=LAM)
             nc.scalar.activation(out=sg[:], in_=xv, func=ACT.Sigmoid)
 
-        def stage_ga(t):
-            s = state[t]
-            u = s["u"]
-            vv = hlp.tile([P, PL], F32, name="vv")
-            s["vv"] = vv
-            nc.gpsimd.tensor_scalar(out=s["t2"][:], in0=s["t2"][:], scalar1=1.0, scalar2=-4.0, op0=ALU.mult, op1=ALU.add)
-            nc.gpsimd.tensor_scalar(
-                out=pl(u, 3), in0=s["y2"][:], scalar1=0.375 * LAM, scalar2=-0.75 * LAM, op0=ALU.mult, op1=ALU.add
-            )
-            nc.gpsimd.tensor_tensor(out=vv[:], in0=s["sn"][:], in1=s["xv"], op=ALU.mult)
-            nc.gpsimd.tensor_tensor(out=pl(u, 7), in0=s["t2"][:], in1=pl(u, 3), op=ALU.mult)
-            nc.gpsimd.tensor_scalar(
-                out=pl(u, 7), in0=pl(u, 7), scalar1=7.0 / 6.0, scalar2=1.75 * LAM, op0=ALU.mult, op1=ALU.add
-            )
+        def stt(o, a, sc, b, op0):
+            nc.vector.scalar_tensor_tensor(out=o, in0=a, scalar=sc, in1=b, op0=op0, op1=ALU.mult)
 
         def stage_va(t, part):
             s = state[t]
             u = s["u"]
             if part == 0:
-                nc.vector.scalar_tensor_tensor(
-                    out=pl(u, 4), in0=s["y2"][:], scalar=4.0, in1=pl(u, 2), op0=ALU.subtract, op1=ALU.mult
-                )
+                stt(pl(u, 7), s["t2"][:], 4.0, pl(u, 3), ALU.subtract)
             elif part == 1:
-                nc.vector.scalar_tensor_tensor(
-                    out=pl(u, 9), in0=pl(u, 5), scalar=0.625, in1=s["t2"][:], op0=ALU.subtract, op1=ALU.mult
-                )
+                stt(pl(u, 9), s["t2"][:], 4.0, pl(u, 5), ALU.subtract)
             elif part == 2:
-                nc.vector.scalar_tensor_tensor(
-                    out=pl(u, 6), in0=s["t2"][:], scalar=2.0, in1=pl(u, 2), op0=ALU.add, op1=ALU.mult
-                )
+                stt(pl(u, 4), s["y2"][:], 4.0, pl(u, 2), ALU.subtract)
+            elif part == 3:
+                stt(pl(u, 8), s["t2"][:], 4.0, pl(u, 4), ALU.subtract)
+            elif part == 4:
+                stt(pl(u, 6), s["t2"][:], 2.0, pl(u, 2), ALU.subtract)
             else:
                 sp = hlp.tile([P, PL], F32, name="sp")
                 s["sp"] = sp
-                nc.vector.scalar_tensor_tensor(
-                    out=sp[:], in0=s["vv"][:], scalar=1.0, in1=s["sg"][:], op0=ALU.add, op1=ALU.mult
-                )
+                stt(sp[:], s["vv"][:], 1.0, s["sg"][:], ALU.add)
 
-        def stage_gb(t):
-            s = state[t]
-            u = s["u"]
-            nc.gpsimd.tensor_tensor(out=pl(u, 8), in0=s["t2"][:], in1=pl(u, 4), op=ALU.mult)
-            nc.gpsimd.tensor_scalar(
-                out=pl(u, 9), in0=pl(u, 9), scalar1=2.25 * LAM, scalar2=-2.25 * LAM, op0=ALU.mult, op1=ALU.add
-            )
+        def stage_sb(t):
+            u = state[t]["u"]
+            nc.scalar.activation(out=pl(u, 7), in_=pl(u, 7), func=ACT.Identity, scale=7.0 / 6.0, bias=1.75 * LAM)
+            nc.scalar.activation(out=pl(u, 9), in_=pl(u, 9), func=ACT.Identity, scale=2.25 * LAM, bias=-2.25 * LAM)
 
         stage_sa(0)
-        stage_ga(0)
         wcs = {}
 
         def new_w(it):
@@ -240,33 +215,32 @@ def tile_kantlinear_kernel(tc, x, base_weight, cheby_weight, grad_out, out):
         regroup(wcs[0][2], raws[0], 0, 512, "v")
         regroup(wcs[0][2], raws[0], 512, 1280, "s")
         quant(wcs[0][0], wcs[0][1], wcs[0][2], 0, 512, E4)
-        for part in range(3):
+        for part in range(5):
             stage_va(0, part)
-        stage_gb(0)
+        stage_sb(0)
         quant(wcs[0][0], wcs[0][1], wcs[0][2], 512, 1024, E4)
         quant(wcs[0][0], wcs[0][1], wcs[0][2], 1024, 1280, E4)
-        stage_va(0, 3)
+        stage_va(0, 5)
         raws.append(load_w(2))
         stage_sa(1)
-        stage_ga(1)
         bgrp = grpp.tile([P, 512, 4], BF16, name="bgrp", tag="grp", align_bytes=64)
         regroup(bgrp, braw, 0, 512, "s")
         bcodes = keep.tile([P, 512], U32, name="bcodes", align_bytes=64)
         bscales = keep.tile([P, 512], U8, name="bscales", align_bytes=64)
         raws.append(load_w(3))
 
-        jobs = [(h, j) for h in range(8) for j in range(11)]
+        jobs = [(h, j) for h in range(8) for j in range(NJ)]
         banks = {}
 
         def emit_mx(h, j):
             ps = pmx.tile([P, 512], F32, name="ps", tag="ps")
             banks[(h, j)] = ps
             it, par = divmod(h, 2)
-            if j == 10:
+            if j == NJ - 1:
                 codes, scales, col, g0 = bcodes, bscales, it * P, 512 * par
             else:
                 codes, scales = wcs[it][0], wcs[it][1]
-                col, g0 = (5 * par + j // 2) * P, 1024 + 512 * (j % 2)
+                col, g0 = (5 * par + j // 3) * P, 1024 + 512 * (j % 3)
             nc.tensor.matmul_mx(
                 out=ps[:],
                 lhsT=codes[:, col : col + P].bitcast(E4),
@@ -280,7 +254,7 @@ def tile_kantlinear_kernel(tc, x, base_weight, cheby_weight, grad_out, out):
         def consume(h, j):
             ps = banks[(h, j)]
             u = state[h]["u"]
-            if j == 10:
+            if j == NJ - 1:
                 p0 = pl(u, 0).rearrange("p (b j) -> p b j", b=5)
                 spv = state[h]["sp"][:].rearrange("p (b j) -> p b j", b=5)
                 nc.vector.tensor_tensor(
@@ -296,24 +270,28 @@ def tile_kantlinear_kernel(tc, x, base_weight, cheby_weight, grad_out, out):
                     op=ALU.mult,
                 )
                 return
-            c = 2 * (j // 2) + h % 2
-            wi = j % 2
+            c = 2 * (j // 3) + h % 2
+            wi = j % 3
+            if wi == 2:
+                a = seg_addr(5, c)
+                d5 = u[:, 1, a : a + J]
+                nc.vector.tensor_tensor(out=d5, in0=d5, in1=ps[:, 0:J], op=ALU.mult)
+                return
             for k in range(2):
                 n = WINDOWS[wi][2 * k]
                 a = n * PL + seg_addr(n, c)
                 dst = u[:, :, a : a + J]
                 src = ps[:, 2 * J * k : 2 * J * k + 2 * J].rearrange("p (e j) -> p e j", e=2)
-                kap = (0.6 if n == 1 else 0.4) / LAM
-                nc.vector.scalar_tensor_tensor(out=dst, in0=dst, scalar=kap, in1=src, op0=ALU.mult, op1=ALU.mult)
-            a = seg_addr(5, c) + 52 * wi
-            d5 = u[:, 1, a : a + 52]
-            nc.vector.scalar_tensor_tensor(
-                out=d5, in0=d5, scalar=0.625, in1=ps[:, 416:468], op0=ALU.subtract, op1=ALU.mult
-            )
+                stt(dst, dst, (0.6 if n == 1 else 0.4) / LAM, src, ALU.mult)
+
+        def pair_sums(h, eng):
+            u = state[h]["u"]
+            for v in range(5):
+                eng.tensor_tensor(out=pl(u, v), in0=pl(u, v), in1=pl(u, 5 + v), op=ALU.add)
 
         acc = {}
-        order = [(n, b) for n in range(10) for b in (0, 1, 2)] + [(n, b) for n in range(10) for b in (3, 4)]
-        cuts = (0, 15, 30, 40, 50)
+        order = [(v, b) for v in range(5) for b in (0, 1, 2)] + [(v, b) for v in range(5) for b in (3, 4)]
+        cuts = (0, 9, 25)
 
         def bunch(h, i):
             u = state[h]["u"]
@@ -321,20 +299,19 @@ def tile_kantlinear_kernel(tc, x, base_weight, cheby_weight, grad_out, out):
                 acc[h] = [pac.tile([P, 2, P], F32, name="pa%d" % b) for b in range(3)]
                 state[h]["ot"] = otp.tile([P, 5, P], F32, name="ot")
             pas = acc[h]
-            for n, bp in order[cuts[i] : cuts[i + 1]]:
-                a = (n % 5) * PL + J * bp
+            for v, bp in order[cuts[i] : cuts[i + 1]]:
+                a = v * PL + J * bp
                 nc.tensor.matmul(
                     out=pas[bp % 3][:, bp // 3, :],
-                    lhsT=u[:, n // 5, a : a + P],
+                    lhsT=u[:, 0, a : a + P],
                     rhs=ident_f[:],
                     is_transpose=True,
-                    start=(n == 0),
-                    stop=(n == 9),
+                    start=(v == 0),
+                    stop=(v == 4),
                 )
             ot = state[h]["ot"]
             if i == 1:
                 nc.scalar.copy(out=ot[:, 2:3, :], in_=pas[2][:, 0:1, :])
-            if i == 3:
                 nc.scalar.copy(out=ot[:, 0:4:3, :], in_=pas[0][:])
                 nc.scalar.copy(out=ot[:, 1:5:3, :], in_=pas[1][:])
                 it, par = divmod(h, 2)
@@ -360,25 +337,28 @@ def tile_kantlinear_kernel(tc, x, base_weight, cheby_weight, grad_out, out):
             h, j = jobs[q]
             consume(h, j)
             it, par = divmod(h, 2)
+            if j == 0 and h > 0:
+                pair_sums(h - 1, nc.gpsimd)
             if j == 0 and h + 2 < 8:
                 stage_sa(h + 2)
             if h + 1 < 8:
-                if j in (1, 3, 5, 7):
-                    stage_va(h + 1, (j - 1) // 2)
-                if j == 4:
-                    stage_gb(h + 1)
-            if j == 6 and h + 2 < 8:
-                stage_ga(h + 2)
+                if j % 2 == 0 and j < 12:
+                    stage_va(h + 1, j // 2)
+                if j == 5:
+                    stage_sb(h + 1)
             if it < 3:
-                if par == 0 and j == 2:
+                if par == 0 and j == 3:
                     new_w(it + 1)
                     regroup(wcs[it + 1][2], raws[it + 1], 0, 640, "s")
-                if par == 0 and j == 7:
+                if par == 0 and j == 9:
                     regroup(wcs[it + 1][2], raws[it + 1], 640, 1280, "s")
-                if par == 1 and j in (0, 2, 4):
+                if par == 1 and j in (1, 3, 5):
                     c0, c1 = ((0, 512), (512, 1024), (1024, 1280))[j // 2]
                     quant(wcs[it + 1][0], wcs[it + 1][1], wcs[it + 1][2], c0, c1, E4)
-            if h > 0 and j in (1, 3, 5, 7):
-                bunch(h - 1, (j - 1) // 2)
-        for i in range(4):
-            bunch(7, i)
+            if h > 0 and j == 9:
+                bunch(h - 1, 0)
+            if h > 0 and j == 14:
+                bunch(h - 1, 1)
+        pair_sums(7, nc.vector)
+        bunch(7, 0)
+        bunch(7, 1)

@@ -20,7 +20,7 @@ J = 104
 PL = 5 * J
 EP = 5 * PL + 32
 LAM = 0.375
-LOOK = 4
+LOOK = 5
 NJ = 16
 WINDOWS = ((1, 6, 2, 7), (3, 8, 4, 9))
 
@@ -51,8 +51,8 @@ def tile_kantlinear_kernel(tc, x, base_weight, cheby_weight, grad_out, out):
         upl = ctx.enter_context(tc.tile_pool(name="upl", bufs=4))
         hlp = ctx.enter_context(tc.tile_pool(name="hlp", bufs=2))
         otp = ctx.enter_context(tc.tile_pool(name="otp", bufs=2))
-        pmx = ctx.enter_context(tc.psum_pool(name="pmx", bufs=5))
-        pac = ctx.enter_context(tc.psum_pool(name="pac", bufs=1))
+        pmx = ctx.enter_context(tc.psum_pool(name="pmx", bufs=6))
+        pac = ctx.enter_context(tc.psum_pool(name="pac", bufs=2))
         ctx.enter_context(tc.manual_schedule())
 
         ident_f = const.tile([P, P], F32, name="ident_f")
@@ -156,14 +156,10 @@ def tile_kantlinear_kernel(tc, x, base_weight, cheby_weight, grad_out, out):
             y2 = hlp.tile([P, PL], F32, name="y2")
             t2 = hlp.tile([P, PL], F32, name="t2")
             sg = hlp.tile([P, PL], F32, name="sg")
-            sn = hlp.tile([P, PL], F32, name="sn")
-            vv = hlp.tile([P, PL], F32, name="vv")
-            state[t] = {"u": u, "xv": xv, "y2": y2, "t2": t2, "sg": sg, "sn": sn, "vv": vv}
+            state[t] = {"u": u, "xv": xv, "y2": y2, "t2": t2, "sg": sg}
             nc.gpsimd.memset(u[:, :, 5 * PL : EP], 0.0)
             nc.gpsimd.memset(pl(u, 0), 0.0)
             nc.gpsimd.memset(pl(u, 1), LAM / 6.0)
-            nc.scalar.activation(out=sn[:], in_=xv, func=ACT.Sigmoid, scale=-1.0)
-            nc.gpsimd.tensor_tensor(out=vv[:], in0=sn[:], in1=xv, op=ALU.mult)
             nc.scalar.activation(out=y2[:], in_=xv, func=ACT.Square, scale=math.sqrt(8.0))
             nc.scalar.activation(
                 out=t2[:], in_=y2[:], func=ACT.Square, scale=math.sqrt(2.0) / 2.0, bias=-2.0 * math.sqrt(2.0)
@@ -192,10 +188,14 @@ def tile_kantlinear_kernel(tc, x, base_weight, cheby_weight, grad_out, out):
                 stt(pl(u, 8), s["t2"][:], 4.0, pl(u, 4), ALU.subtract)
             elif part == 4:
                 stt(pl(u, 6), s["t2"][:], 2.0, pl(u, 2), ALU.subtract)
+            elif part == 5:
+                vv = hlp.tile([P, PL], F32, name="vv")
+                s["vv"] = vv
+                stt(vv[:], s["sg"][:], 1.0, s["xv"], ALU.subtract)
             else:
                 sp = hlp.tile([P, PL], F32, name="sp")
                 s["sp"] = sp
-                stt(sp[:], s["vv"][:], 1.0, s["sg"][:], ALU.add)
+                stt(sp[:], s["vv"][:], 1.0, s["sg"][:], ALU.subtract)
 
         def stage_sb(t):
             u = state[t]["u"]
@@ -221,6 +221,7 @@ def tile_kantlinear_kernel(tc, x, base_weight, cheby_weight, grad_out, out):
         quant(wcs[0][0], wcs[0][1], wcs[0][2], 512, 1024, E4)
         quant(wcs[0][0], wcs[0][1], wcs[0][2], 1024, 1280, E4)
         stage_va(0, 5)
+        stage_va(0, 6)
         raws.append(load_w(2))
         stage_sa(1)
         bgrp = grpp.tile([P, 512, 4], BF16, name="bgrp", tag="grp", align_bytes=64)
@@ -257,17 +258,13 @@ def tile_kantlinear_kernel(tc, x, base_weight, cheby_weight, grad_out, out):
             if j == NJ - 1:
                 p0 = pl(u, 0).rearrange("p (b j) -> p b j", b=5)
                 spv = state[h]["sp"][:].rearrange("p (b j) -> p b j", b=5)
-                nc.vector.tensor_tensor(
-                    out=p0[:, :, 0:102],
-                    in0=spv[:, :, 0:102],
-                    in1=ps[:, 0:510].rearrange("p (j b) -> p b j", b=5),
-                    op=ALU.mult,
-                )
-                nc.vector.tensor_tensor(
-                    out=p0[:, 0:2, 102:103],
-                    in0=spv[:, 0:2, 102:103],
-                    in1=ps[:, 510:512].rearrange("p (j b) -> p b j", b=2),
-                    op=ALU.mult,
+                stt(p0[:, :, 0:102], spv[:, :, 0:102], -1.0, ps[:, 0:510].rearrange("p (j b) -> p b j", b=5), ALU.mult)
+                stt(
+                    p0[:, 0:2, 102:103],
+                    spv[:, 0:2, 102:103],
+                    -1.0,
+                    ps[:, 510:512].rearrange("p (j b) -> p b j", b=2),
+                    ALU.mult,
                 )
                 return
             c = 2 * (j // 3) + h % 2
@@ -284,36 +281,30 @@ def tile_kantlinear_kernel(tc, x, base_weight, cheby_weight, grad_out, out):
                 src = ps[:, 2 * J * k : 2 * J * k + 2 * J].rearrange("p (e j) -> p e j", e=2)
                 stt(dst, dst, (0.6 if n == 1 else 0.4) / LAM, src, ALU.mult)
 
-        def pair_sums(h, eng):
-            u = state[h]["u"]
-            for v in range(5):
-                eng.tensor_tensor(out=pl(u, v), in0=pl(u, v), in1=pl(u, 5 + v), op=ALU.add)
-
         acc = {}
-        order = [(v, b) for v in range(5) for b in (0, 1, 2)] + [(v, b) for v in range(5) for b in (3, 4)]
-        cuts = (0, 9, 25)
 
-        def bunch(h, i):
+        def bunch(h, bp):
             u = state[h]["u"]
-            if i == 0:
-                acc[h] = [pac.tile([P, 2, P], F32, name="pa%d" % b) for b in range(3)]
+            if bp == 0 or bp == 3:
+                acc[h] = pac.tile([P, 4, P], F32, name="pa")
+            if bp == 0:
                 state[h]["ot"] = otp.tile([P, 5, P], F32, name="ot")
-            pas = acc[h]
-            for v, bp in order[cuts[i] : cuts[i + 1]]:
-                a = v * PL + J * bp
+            pa = acc[h]
+            for n in range(10):
+                a = (n % 5) * PL + J * bp
                 nc.tensor.matmul(
-                    out=pas[bp % 3][:, bp // 3, :],
-                    lhsT=u[:, 0, a : a + P],
+                    out=pa[:, bp % 3, :],
+                    lhsT=u[:, n // 5, a : a + P],
                     rhs=ident_f[:],
                     is_transpose=True,
-                    start=(v == 0),
-                    stop=(v == 4),
+                    start=(n == 0),
+                    stop=(n == 9),
                 )
             ot = state[h]["ot"]
-            if i == 1:
-                nc.scalar.copy(out=ot[:, 2:3, :], in_=pas[2][:, 0:1, :])
-                nc.scalar.copy(out=ot[:, 0:4:3, :], in_=pas[0][:])
-                nc.scalar.copy(out=ot[:, 1:5:3, :], in_=pas[1][:])
+            if bp == 2:
+                nc.scalar.copy(out=ot[:, 0:3, :], in_=pa[:, 0:3, :])
+            if bp == 4:
+                nc.scalar.copy(out=ot[:, 3:5, :], in_=pa[:, 0:2, :])
                 it, par = divmod(h, 2)
                 cols = slice(it * P, (it + 1) * P)
                 nc.sync.dma_start(
@@ -337,12 +328,10 @@ def tile_kantlinear_kernel(tc, x, base_weight, cheby_weight, grad_out, out):
             h, j = jobs[q]
             consume(h, j)
             it, par = divmod(h, 2)
-            if j == 0 and h > 0:
-                pair_sums(h - 1, nc.gpsimd)
             if j == 0 and h + 2 < 8:
                 stage_sa(h + 2)
             if h + 1 < 8:
-                if j % 2 == 0 and j < 12:
+                if j % 2 == 0 and j < 14:
                     stage_va(h + 1, j // 2)
                 if j == 5:
                     stage_sb(h + 1)
@@ -355,10 +344,7 @@ def tile_kantlinear_kernel(tc, x, base_weight, cheby_weight, grad_out, out):
                 if par == 1 and j in (1, 3, 5):
                     c0, c1 = ((0, 512), (512, 1024), (1024, 1280))[j // 2]
                     quant(wcs[it + 1][0], wcs[it + 1][1], wcs[it + 1][2], c0, c1, E4)
-            if h > 0 and j == 9:
-                bunch(h - 1, 0)
-            if h > 0 and j == 14:
-                bunch(h - 1, 1)
-        pair_sums(7, nc.vector)
-        bunch(7, 0)
-        bunch(7, 1)
+            if h > 0 and j % 3 == 2:
+                bunch(h - 1, j // 3)
+        for bp in range(5):
+            bunch(7, bp)

@@ -91,7 +91,7 @@ def tile_kantlinear_kernel(tc, x, base_weight, cheby_weight, grad_out, out):
         gs = rawp.tile([P, 8, 512], BF16, name="gs", tag="raw")
         nc.sync.dma_start(out=gs[:], in_=grad_out.rearrange("(t p) k -> p t k", p=P))
         xs = rawp.tile([P, 10, 512], BF16, name="xs", tag="raw")
-        nc.gpsimd.memset(xs[96:128], 0.0)
+        nc.vector.memset(xs[96:128].bitcast(F32), 0.0)
         nc.sync.dma_start(out=xs[0:96], in_=x[0:960, :].rearrange("(j r) i -> j r i", r=10))
         nc.sync.dma_start(out=xs[96:102], in_=x[960:1020, :].rearrange("(j r) i -> j r i", r=10))
         nc.sync.dma_start(out=xs[102:103, 0:4, :], in_=x[1020:1024, :].rearrange("(o r) i -> o r i", o=1))
@@ -157,9 +157,6 @@ def tile_kantlinear_kernel(tc, x, base_weight, cheby_weight, grad_out, out):
             t2 = hlp.tile([P, PL], F32, name="t2")
             sg = hlp.tile([P, PL], F32, name="sg")
             state[t] = {"u": u, "xv": xv, "y2": y2, "t2": t2, "sg": sg}
-            nc.gpsimd.memset(u[:, :, 5 * PL : EP], 0.0)
-            nc.gpsimd.memset(pl(u, 0), 0.0)
-            nc.gpsimd.memset(pl(u, 1), LAM / 6.0)
             nc.scalar.activation(out=y2[:], in_=xv, func=ACT.Square, scale=math.sqrt(8.0))
             nc.scalar.activation(
                 out=t2[:], in_=y2[:], func=ACT.Square, scale=math.sqrt(2.0) / 2.0, bias=-2.0 * math.sqrt(2.0)
@@ -171,6 +168,12 @@ def tile_kantlinear_kernel(tc, x, base_weight, cheby_weight, grad_out, out):
             nc.scalar.activation(out=pl(u, 5), in_=pl(u, 5), func=ACT.Identity, scale=1.0, bias=-0.625)
             nc.scalar.activation(out=pl(u, 2), in_=xv, func=ACT.Copy, scale=LAM)
             nc.scalar.activation(out=sg[:], in_=xv, func=ACT.Sigmoid)
+
+        def stage_vm(t):
+            u = state[t]["u"]
+            nc.vector.memset(u[:, :, 5 * PL : EP], 0.0)
+            nc.vector.memset(pl(u, 0).rearrange("p (b j) -> p b j", b=5)[:, :, 102:104], 0.0)
+            nc.vector.memset(pl(u, 1), LAM / 6.0)
 
         def stt(o, a, sc, b, op0):
             nc.vector.scalar_tensor_tensor(out=o, in0=a, scalar=sc, in1=b, op0=op0, op1=ALU.mult)
@@ -203,6 +206,7 @@ def tile_kantlinear_kernel(tc, x, base_weight, cheby_weight, grad_out, out):
             nc.scalar.activation(out=pl(u, 9), in_=pl(u, 9), func=ACT.Identity, scale=2.25 * LAM, bias=-2.25 * LAM)
 
         stage_sa(0)
+        stage_vm(0)
         wcs = {}
 
         def new_w(it):
@@ -224,6 +228,7 @@ def tile_kantlinear_kernel(tc, x, base_weight, cheby_weight, grad_out, out):
         stage_va(0, 6)
         raws.append(load_w(2))
         stage_sa(1)
+        stage_vm(1)
         bgrp = grpp.tile([P, 512, 4], BF16, name="bgrp", tag="grp", align_bytes=64)
         regroup(bgrp, braw, 0, 512, "s")
         bcodes = keep.tile([P, 512], U32, name="bcodes", align_bytes=64)
@@ -283,14 +288,14 @@ def tile_kantlinear_kernel(tc, x, base_weight, cheby_weight, grad_out, out):
 
         acc = {}
 
-        def bunch(h, bp):
+        def bunch(h, bp, planes=10):
             u = state[h]["u"]
             if bp == 0 or bp == 3:
                 acc[h] = pac.tile([P, 4, P], F32, name="pa")
             if bp == 0:
                 state[h]["ot"] = otp.tile([P, 5, P], F32, name="ot")
             pa = acc[h]
-            for n in range(10):
+            for n in range(planes):
                 a = (n % 5) * PL + J * bp
                 nc.tensor.matmul(
                     out=pa[:, bp % 3, :],
@@ -298,7 +303,7 @@ def tile_kantlinear_kernel(tc, x, base_weight, cheby_weight, grad_out, out):
                     rhs=ident_f[:],
                     is_transpose=True,
                     start=(n == 0),
-                    stop=(n == 9),
+                    stop=(n == planes - 1),
                 )
             ot = state[h]["ot"]
             if bp == 2:
@@ -330,6 +335,8 @@ def tile_kantlinear_kernel(tc, x, base_weight, cheby_weight, grad_out, out):
             it, par = divmod(h, 2)
             if j == 0 and h + 2 < 8:
                 stage_sa(h + 2)
+            if j == 3 and h + 2 < 8:
+                stage_vm(h + 2)
             if h + 1 < 8:
                 if j % 2 == 0 and j < 14:
                     stage_va(h + 1, j // 2)
@@ -346,5 +353,11 @@ def tile_kantlinear_kernel(tc, x, base_weight, cheby_weight, grad_out, out):
                     quant(wcs[it + 1][0], wcs[it + 1][1], wcs[it + 1][2], c0, c1, E4)
             if h > 0 and j % 3 == 2:
                 bunch(h - 1, j // 3)
-        for bp in range(5):
+        ul = state[7]["u"][:, :, 0 : 5 * PL].rearrange("p e (v r) -> p e v r", v=5)
+        nc.vector.tensor_tensor(
+            out=ul[:, 0, :, 3 * J : PL], in0=ul[:, 0, :, 3 * J : PL], in1=ul[:, 1, :, 3 * J : PL], op=ALU.add
+        )
+        for bp in range(3):
             bunch(7, bp)
+        for bp in (3, 4):
+            bunch(7, bp, 5)

@@ -18,11 +18,12 @@ FLOPS = 2 * 1024 * 512 * 5632
 P = 128
 J = 104
 PL = 5 * J
-EP = 5 * PL + 32
-LAM = 0.375
-LOOK = 5
-NJ = 16
-WINDOWS = ((1, 6, 2, 7), (3, 8, 4, 9))
+EP = 2920
+LAM = 0.4
+LOOK = 4
+CHUNKS = (0, 2, 4, 6, 8, 1, 3, 5, 7, 9)
+WINDOWS = ((1, 2, 6, 7), (3, 4, 8, 9))
+SLOT = (4, 0, 1, 2, 3)
 
 
 def theta(n):
@@ -51,8 +52,9 @@ def tile_kantlinear_kernel(tc, x, base_weight, cheby_weight, grad_out, out):
         upl = ctx.enter_context(tc.tile_pool(name="upl", bufs=4))
         hlp = ctx.enter_context(tc.tile_pool(name="hlp", bufs=2))
         otp = ctx.enter_context(tc.tile_pool(name="otp", bufs=2))
-        pmx = ctx.enter_context(tc.psum_pool(name="pmx", bufs=6))
-        pac = ctx.enter_context(tc.psum_pool(name="pac", bufs=2))
+        tlp = ctx.enter_context(tc.tile_pool(name="tlp", bufs=1))
+        pmx = ctx.enter_context(tc.psum_pool(name="pmx", bufs=5))
+        pac = ctx.enter_context(tc.psum_pool(name="pac", bufs=1))
         ctx.enter_context(tc.manual_schedule())
 
         ident_f = const.tile([P, P], F32, name="ident_f")
@@ -81,15 +83,19 @@ def tile_kantlinear_kernel(tc, x, base_weight, cheby_weight, grad_out, out):
             else:
                 nc.scalar.copy(out=d, in_=s)
 
-        def quant(codes, scales, grp, c0, c1, fmt, g0=0):
+        def quant(codes, scales, grp, c0, c1, fmt):
             nc.vector.quantize_mx(
-                out=codes[:, g0 + c0 : g0 + c1].bitcast(fmt),
-                scales=scales[:, g0 + c0 : g0 + c1],
+                out=codes[:, c0:c1].bitcast(fmt),
+                scales=scales[:, c0:c1],
                 in_=grp[:, c0:c1, :].rearrange("p r t -> p (r t)"),
             )
 
         gs = rawp.tile([P, 8, 512], BF16, name="gs", tag="raw")
-        nc.sync.dma_start(out=gs[:], in_=grad_out.rearrange("(t p) k -> p t k", p=P))
+        for q in range(4):
+            nc.sync.dma_start(
+                out=gs[:, 2 * q : 2 * q + 2, :],
+                in_=grad_out[256 * q : 256 * q + 256, :].rearrange("(t p) k -> p t k", p=P),
+            )
         xs = rawp.tile([P, 10, 512], BF16, name="xs", tag="raw")
         nc.vector.memset(xs[96:128].bitcast(F32), 0.0)
         nc.sync.dma_start(out=xs[0:96], in_=x[0:960, :].rearrange("(j r) i -> j r i", r=10))
@@ -116,7 +122,7 @@ def tile_kantlinear_kernel(tc, x, base_weight, cheby_weight, grad_out, out):
         )
         ge = grpp.tile([P, 1024, 4], BF16, name="ge", tag="grp", align_bytes=64)
         ge32 = ge[:].bitcast(F32)
-        gw = grpp.tile([P, 1536, 4], BF16, name="gw", tag="grp", align_bytes=64)
+        gw = grpp.tile([P, 1024, 4], BF16, name="gw", tag="grp", align_bytes=64)
         gw32 = gw[:].bitcast(F32)
         for wi, ns in enumerate(WINDOWS):
             for k, n in enumerate(ns):
@@ -124,15 +130,24 @@ def tile_kantlinear_kernel(tc, x, base_weight, cheby_weight, grad_out, out):
                 nc.vector.tensor_copy(
                     out=gw32[:, 512 * wi + J * k : 512 * wi + J * k + J, :], in_=gn32[:, s : s + J, :]
                 )
-            nc.vector.memset(gw32[:, 512 * wi + 416 : 512 * wi + 512, :], 0.0)
-        nc.vector.tensor_copy(out=gw32[:, 1024:1536, :], in_=gn32[:, 512:1024, :])
-        gcodes = keep.tile([P, 2560], U32, name="gcodes", align_bytes=64)
-        gscales = keep.tile([P, 2560], U8, name="gscales", align_bytes=64)
-        quant(gcodes, gscales, gw, 0, 1024, E5, 1024)
-        quant(gcodes, gscales, gw, 1024, 1536, E5, 1024)
+            nc.vector.tensor_copy(
+                out=gw32[:, 512 * wi + 416 : 512 * wi + 468, :], in_=gn32[:, 512 + 52 * wi : 564 + 52 * wi, :]
+            )
+            nc.vector.memset(gw32[:, 512 * wi + 468 : 512 * wi + 512, :], 0.0)
+        gcodes = keep.tile([P, 2048], U32, name="gcodes", align_bytes=64)
+        gscales = keep.tile([P, 2048], U8, name="gscales", align_bytes=64)
+        nc.vector.quantize_mx(
+            out=gcodes[:, 1024:2048].bitcast(E5),
+            scales=gscales[:, 1024:2048],
+            in_=gw[:].rearrange("p r t -> p (r t)"),
+        )
         for par in range(2):
             nc.vector.tensor_copy(out=ge32[:, 512 * par : 512 * par + 512, :], in_=gn32[:, par:1024:2, :])
-        quant(gcodes, gscales, ge, 0, 1024, E5)
+        nc.vector.quantize_mx(
+            out=gcodes[:, 0:1024].bitcast(E5),
+            scales=gscales[:, 0:1024],
+            in_=ge[:].rearrange("p r t -> p (r t)"),
+        )
 
         xT = keep.tile([P, 40, J], BF16, name="xT")
         for grp in range(5):
@@ -148,7 +163,7 @@ def tile_kantlinear_kernel(tc, x, base_weight, cheby_weight, grad_out, out):
         state = {}
 
         def pl(u, n):
-            return u[:, n // 5, (n % 5) * PL : (n % 5) * PL + PL]
+            return u[:, n // 5, SLOT[n % 5] * PL : SLOT[n % 5] * PL + PL]
 
         def stage_sa(t):
             u = upl.tile([P, 2, EP], F32, name="u")
@@ -156,57 +171,73 @@ def tile_kantlinear_kernel(tc, x, base_weight, cheby_weight, grad_out, out):
             y2 = hlp.tile([P, PL], F32, name="y2")
             t2 = hlp.tile([P, PL], F32, name="t2")
             sg = hlp.tile([P, PL], F32, name="sg")
-            state[t] = {"u": u, "xv": xv, "y2": y2, "t2": t2, "sg": sg}
+            sn = hlp.tile([P, PL], F32, name="sn")
+            z3 = hlp.tile([P, PL], F32, name="z3")
+            state[t] = {"u": u, "xv": xv, "y2": y2, "t2": t2, "sg": sg, "sn": sn, "z3": z3}
+            nc.gpsimd.memset(u[:, :, 5 * PL : 5 * PL + 32], 0.0)
+            nc.gpsimd.memset(pl(u, 0), 0.0)
             nc.scalar.activation(out=y2[:], in_=xv, func=ACT.Square, scale=math.sqrt(8.0))
             nc.scalar.activation(
                 out=t2[:], in_=y2[:], func=ACT.Square, scale=math.sqrt(2.0) / 2.0, bias=-2.0 * math.sqrt(2.0)
             )
-            nc.scalar.activation(out=pl(u, 3), in_=y2[:], func=ACT.Identity, scale=0.375 * LAM, bias=-0.75 * LAM)
+            nc.scalar.activation(out=sn[:], in_=xv, func=ACT.Sigmoid, scale=-1.0)
+            nc.scalar.activation(out=pl(u, 2), in_=xv, func=ACT.Copy, scale=LAM)
             nc.scalar.activation(
                 out=pl(u, 5), in_=y2[:], func=ACT.Square, scale=math.sqrt(0.5) / 2.0, bias=-1.5 * math.sqrt(0.5)
             )
-            nc.scalar.activation(out=pl(u, 5), in_=pl(u, 5), func=ACT.Identity, scale=1.0, bias=-0.625)
-            nc.scalar.activation(out=pl(u, 2), in_=xv, func=ACT.Copy, scale=LAM)
+            nc.scalar.activation(
+                out=z3[:], in_=y2[:], func=ACT.Square, scale=math.sqrt(3.0) / 2.0, bias=-2.0 * math.sqrt(3.0)
+            )
             nc.scalar.activation(out=sg[:], in_=xv, func=ACT.Sigmoid)
+            nc.scalar.activation(out=pl(u, 1), in_=xv, func=ACT.Identity, scale=0.0, bias=0.1)
 
-        def stage_vm(t):
-            u = state[t]["u"]
-            nc.vector.memset(u[:, :, 5 * PL : EP], 0.0)
-            nc.vector.memset(pl(u, 0).rearrange("p (b j) -> p b j", b=5)[:, :, 102:104], 0.0)
-            nc.vector.memset(pl(u, 1), LAM / 6.0)
-
-        def stt(o, a, sc, b, op0):
-            nc.vector.scalar_tensor_tensor(out=o, in0=a, scalar=sc, in1=b, op0=op0, op1=ALU.mult)
+        def stage_ga(t):
+            s = state[t]
+            u = s["u"]
+            vv = s["sn"]
+            s["vv"] = vv
+            nc.gpsimd.tensor_scalar(out=s["t2"][:], in0=s["t2"][:], scalar1=1.0, scalar2=-4.0, op0=ALU.mult, op1=ALU.add)
+            nc.gpsimd.tensor_scalar(
+                out=pl(u, 3), in0=s["y2"][:], scalar1=0.375 * LAM, scalar2=-0.75 * LAM, op0=ALU.mult, op1=ALU.add
+            )
+            nc.gpsimd.tensor_tensor(out=vv[:], in0=s["sn"][:], in1=s["xv"], op=ALU.mult)
+            nc.gpsimd.tensor_tensor(out=pl(u, 7), in0=s["t2"][:], in1=pl(u, 3), op=ALU.mult)
+            nc.gpsimd.tensor_scalar(
+                out=pl(u, 7), in0=pl(u, 7), scalar1=7.0 / 6.0, scalar2=1.75 * LAM, op0=ALU.mult, op1=ALU.add
+            )
 
         def stage_va(t, part):
             s = state[t]
             u = s["u"]
             if part == 0:
-                stt(pl(u, 7), s["t2"][:], 4.0, pl(u, 3), ALU.subtract)
+                nc.vector.scalar_tensor_tensor(
+                    out=pl(u, 4), in0=s["y2"][:], scalar=4.0, in1=pl(u, 2), op0=ALU.subtract, op1=ALU.mult
+                )
             elif part == 1:
-                stt(pl(u, 9), s["t2"][:], 4.0, pl(u, 5), ALU.subtract)
+                nc.vector.scalar_tensor_tensor(
+                    out=pl(u, 9), in0=pl(u, 5), scalar=0.625, in1=s["t2"][:], op0=ALU.subtract, op1=ALU.mult
+                )
             elif part == 2:
-                stt(pl(u, 4), s["y2"][:], 4.0, pl(u, 2), ALU.subtract)
-            elif part == 3:
-                stt(pl(u, 8), s["t2"][:], 4.0, pl(u, 4), ALU.subtract)
-            elif part == 4:
-                stt(pl(u, 6), s["t2"][:], 2.0, pl(u, 2), ALU.subtract)
-            elif part == 5:
-                vv = hlp.tile([P, PL], F32, name="vv")
-                s["vv"] = vv
-                stt(vv[:], s["sg"][:], 1.0, s["xv"], ALU.subtract)
+                nc.vector.scalar_tensor_tensor(
+                    out=pl(u, 6), in0=s["z3"][:], scalar=3.0, in1=pl(u, 2), op0=ALU.subtract, op1=ALU.mult
+                )
             else:
                 sp = hlp.tile([P, PL], F32, name="sp")
                 s["sp"] = sp
-                stt(sp[:], s["vv"][:], 1.0, s["sg"][:], ALU.subtract)
+                nc.vector.scalar_tensor_tensor(
+                    out=sp[:], in0=s["vv"][:], scalar=1.0, in1=s["sg"][:], op0=ALU.add, op1=ALU.mult
+                )
 
-        def stage_sb(t):
-            u = state[t]["u"]
-            nc.scalar.activation(out=pl(u, 7), in_=pl(u, 7), func=ACT.Identity, scale=7.0 / 6.0, bias=1.75 * LAM)
-            nc.scalar.activation(out=pl(u, 9), in_=pl(u, 9), func=ACT.Identity, scale=2.25 * LAM, bias=-2.25 * LAM)
+        def stage_gb(t):
+            s = state[t]
+            u = s["u"]
+            nc.gpsimd.tensor_tensor(out=pl(u, 8), in0=s["t2"][:], in1=pl(u, 4), op=ALU.mult)
+            nc.gpsimd.tensor_scalar(
+                out=pl(u, 9), in0=pl(u, 9), scalar1=2.25 * LAM, scalar2=-2.25 * LAM, op0=ALU.mult, op1=ALU.add
+            )
 
         stage_sa(0)
-        stage_vm(0)
+        stage_ga(0)
         wcs = {}
 
         def new_w(it):
@@ -219,34 +250,33 @@ def tile_kantlinear_kernel(tc, x, base_weight, cheby_weight, grad_out, out):
         regroup(wcs[0][2], raws[0], 0, 512, "v")
         regroup(wcs[0][2], raws[0], 512, 1280, "s")
         quant(wcs[0][0], wcs[0][1], wcs[0][2], 0, 512, E4)
-        for part in range(5):
+        for part in range(3):
             stage_va(0, part)
-        stage_sb(0)
+        stage_gb(0)
         quant(wcs[0][0], wcs[0][1], wcs[0][2], 512, 1024, E4)
         quant(wcs[0][0], wcs[0][1], wcs[0][2], 1024, 1280, E4)
-        stage_va(0, 5)
-        stage_va(0, 6)
+        stage_va(0, 3)
         raws.append(load_w(2))
         stage_sa(1)
-        stage_vm(1)
+        stage_ga(1)
         bgrp = grpp.tile([P, 512, 4], BF16, name="bgrp", tag="grp", align_bytes=64)
         regroup(bgrp, braw, 0, 512, "s")
         bcodes = keep.tile([P, 512], U32, name="bcodes", align_bytes=64)
         bscales = keep.tile([P, 512], U8, name="bscales", align_bytes=64)
         raws.append(load_w(3))
 
-        jobs = [(h, j) for h in range(8) for j in range(NJ)]
+        jobs = [(h, j) for h in range(8) for j in range(11)]
         banks = {}
 
         def emit_mx(h, j):
             ps = pmx.tile([P, 512], F32, name="ps", tag="ps")
             banks[(h, j)] = ps
             it, par = divmod(h, 2)
-            if j == NJ - 1:
+            if j == 10:
                 codes, scales, col, g0 = bcodes, bscales, it * P, 512 * par
             else:
                 codes, scales = wcs[it][0], wcs[it][1]
-                col, g0 = (5 * par + j // 3) * P, 1024 + 512 * (j % 3)
+                col, g0 = (5 * par + j // 2) * P, 1024 + 512 * (j % 2)
             nc.tensor.matmul_mx(
                 out=ps[:],
                 lhsT=codes[:, col : col + P].bitcast(E4),
@@ -260,56 +290,62 @@ def tile_kantlinear_kernel(tc, x, base_weight, cheby_weight, grad_out, out):
         def consume(h, j):
             ps = banks[(h, j)]
             u = state[h]["u"]
-            if j == NJ - 1:
+            if j == 10:
                 p0 = pl(u, 0).rearrange("p (b j) -> p b j", b=5)
                 spv = state[h]["sp"][:].rearrange("p (b j) -> p b j", b=5)
-                stt(p0[:, :, 0:102], spv[:, :, 0:102], -1.0, ps[:, 0:510].rearrange("p (j b) -> p b j", b=5), ALU.mult)
-                stt(
-                    p0[:, 0:2, 102:103],
-                    spv[:, 0:2, 102:103],
-                    -1.0,
-                    ps[:, 510:512].rearrange("p (j b) -> p b j", b=2),
-                    ALU.mult,
+                nc.vector.tensor_tensor(
+                    out=p0[:, :, 0:102],
+                    in0=spv[:, :, 0:102],
+                    in1=ps[:, 0:510].rearrange("p (j b) -> p b j", b=5),
+                    op=ALU.mult,
+                )
+                nc.vector.tensor_tensor(
+                    out=p0[:, 0:2, 102:103],
+                    in0=spv[:, 0:2, 102:103],
+                    in1=ps[:, 510:512].rearrange("p (j b) -> p b j", b=2),
+                    op=ALU.mult,
                 )
                 return
-            c = 2 * (j // 3) + h % 2
-            wi = j % 3
-            if wi == 2:
-                a = seg_addr(5, c)
-                d5 = u[:, 1, a : a + J]
-                nc.vector.tensor_tensor(out=d5, in0=d5, in1=ps[:, 0:J], op=ALU.mult)
-                return
-            for k in range(2):
-                n = WINDOWS[wi][2 * k]
-                a = n * PL + seg_addr(n, c)
-                dst = u[:, :, a : a + J]
-                src = ps[:, 2 * J * k : 2 * J * k + 2 * J].rearrange("p (e j) -> p e j", e=2)
-                stt(dst, dst, (0.6 if n == 1 else 0.4) / LAM, src, ALU.mult)
+            c = 2 * (j // 2) + h % 2
+            wi = j % 2
+            na, nb = WINDOWS[wi][0], WINDOWS[wi][1]
+            aa = SLOT[na] * PL + seg_addr(na, c)
+            step = SLOT[nb] * PL + seg_addr(nb, c) - aa
+            dst = u[:, :, aa : aa + 2 * step].rearrange("p e (a d) -> p e a d", a=2)[:, :, :, 0:J]
+            src = ps[:, 0 : 4 * J].rearrange("p (e a j) -> p e a j", e=2, a=2)
+            nc.vector.tensor_tensor(out=dst, in0=dst, in1=src, op=ALU.mult)
+            a = SLOT[0] * PL + seg_addr(5, c) + 52 * wi
+            d5 = u[:, 1, a : a + 52]
+            nc.vector.scalar_tensor_tensor(
+                out=d5, in0=d5, scalar=0.625, in1=ps[:, 416:468], op0=ALU.subtract, op1=ALU.mult
+            )
 
         acc = {}
+        order = [(n, b) for n in range(10) for b in (0, 1, 2)] + [(n, b) for n in range(10) for b in (3, 4)]
+        cuts = (0, 15, 30, 40, 50)
 
-        def bunch(h, bp, planes=10):
+        def bunch(h, i, todo=None, summed=None):
             u = state[h]["u"]
-            if bp == 0 or bp == 3:
-                acc[h] = pac.tile([P, 4, P], F32, name="pa")
-            if bp == 0:
+            if i == 0:
+                acc[h] = [pac.tile([P, 2, P], F32, name="pa%d" % b) for b in range(3)]
                 state[h]["ot"] = otp.tile([P, 5, P], F32, name="ot")
-            pa = acc[h]
-            for n in range(planes):
+            pas = acc[h]
+            for n, bp in order[cuts[i] : cuts[i + 1]] if todo is None else todo:
                 a = (n % 5) * PL + J * bp
                 nc.tensor.matmul(
-                    out=pa[:, bp % 3, :],
-                    lhsT=u[:, n // 5, a : a + P],
+                    out=pas[bp % 3][:, bp // 3, :],
+                    lhsT=u[:, n // 5, a : a + P] if summed is None else summed[:, 0, J * (bp - 2) : J * (bp - 2) + P],
                     rhs=ident_f[:],
                     is_transpose=True,
                     start=(n == 0),
-                    stop=(n == planes - 1),
+                    stop=(n == 9 or summed is not None),
                 )
             ot = state[h]["ot"]
-            if bp == 2:
-                nc.scalar.copy(out=ot[:, 0:3, :], in_=pa[:, 0:3, :])
-            if bp == 4:
-                nc.scalar.copy(out=ot[:, 3:5, :], in_=pa[:, 0:2, :])
+            if i == 1:
+                nc.scalar.copy(out=ot[:, 2:3, :], in_=pas[2][:, 0:1, :])
+            if i == 3:
+                nc.scalar.copy(out=ot[:, 0:4:3, :], in_=pas[0][:])
+                nc.scalar.copy(out=ot[:, 1:5:3, :], in_=pas[1][:])
                 it, par = divmod(h, 2)
                 cols = slice(it * P, (it + 1) * P)
                 nc.sync.dma_start(
@@ -335,29 +371,33 @@ def tile_kantlinear_kernel(tc, x, base_weight, cheby_weight, grad_out, out):
             it, par = divmod(h, 2)
             if j == 0 and h + 2 < 8:
                 stage_sa(h + 2)
-            if j == 3 and h + 2 < 8:
-                stage_vm(h + 2)
             if h + 1 < 8:
-                if j % 2 == 0 and j < 14:
-                    stage_va(h + 1, j // 2)
-                if j == 5:
-                    stage_sb(h + 1)
+                if j in (1, 3, 5, 7):
+                    stage_va(h + 1, (j - 1) // 2)
+                if j == 4:
+                    stage_gb(h + 1)
+            if j == 6 and h + 2 < 8:
+                stage_ga(h + 2)
             if it < 3:
-                if par == 0 and j == 3:
+                if par == 0 and j == 2:
                     new_w(it + 1)
                     regroup(wcs[it + 1][2], raws[it + 1], 0, 640, "s")
-                if par == 0 and j == 9:
+                if par == 0 and j == 7:
                     regroup(wcs[it + 1][2], raws[it + 1], 640, 1280, "s")
-                if par == 1 and j in (1, 3, 5):
+                if par == 1 and j in (0, 2, 4):
                     c0, c1 = ((0, 512), (512, 1024), (1024, 1280))[j // 2]
                     quant(wcs[it + 1][0], wcs[it + 1][1], wcs[it + 1][2], c0, c1, E4)
-            if h > 0 and j % 3 == 2:
-                bunch(h - 1, j // 3)
+            if h > 0 and j in (1, 3, 5, 7):
+                bunch(h - 1, (j - 1) // 2)
         ul = state[7]["u"][:, :, 0 : 5 * PL].rearrange("p e (v r) -> p e v r", v=5)
-        nc.vector.tensor_tensor(
-            out=ul[:, 0, :, 3 * J : PL], in0=ul[:, 0, :, 3 * J : PL], in1=ul[:, 1, :, 3 * J : PL], op=ALU.add
-        )
-        for bp in range(3):
-            bunch(7, bp)
-        for bp in (3, 4):
-            bunch(7, bp, 5)
+        lo = 2 * J
+        wd = PL - lo
+        sc = tlp.tile([P, 5, wd + 32], F32, name="sc")
+        nc.vector.memset(sc[:, 0, wd : wd + 32], 0.0)
+        nc.vector.tensor_tensor(out=sc[:, :, 0:wd], in0=ul[:, 0, :, lo:PL], in1=ul[:, 1, :, lo:PL], op=ALU.add)
+        nc.vector.tensor_tensor(out=sc[:, 0:4:2, 0:wd], in0=sc[:, 0:4:2, 0:wd], in1=sc[:, 1:4:2, 0:wd], op=ALU.add)
+        nc.vector.tensor_tensor(out=sc[:, 0, 0:wd], in0=sc[:, 0, 0:wd], in1=sc[:, 2, 0:wd], op=ALU.add)
+        nc.vector.tensor_tensor(out=sc[:, 0, 0:wd], in0=sc[:, 0, 0:wd], in1=sc[:, 4, 0:wd], op=ALU.add)
+        bunch(7, 0, [(n, b) for n in range(10) for b in (0, 1)])
+        bunch(7, 1, [(0, 2)], sc)
+        bunch(7, 3, [(0, 3), (0, 4)], sc)

import math
from contextlib import ExitStack

import concourse.mybir as mybir
from concourse.masks import make_identity

F32 = mybir.dt.float32
BF16 = mybir.dt.bfloat16
U32 = mybir.dt.uint32
U8 = mybir.dt.uint8
E4 = mybir.dt.float8_e4m3fn_x4
E5 = mybir.dt.float8_e5m2_x4
ALU = mybir.AluOpType
ACT = mybir.ActivationFunctionType

FLOPS = 2 * 1024 * 512 * 5632

P = 128
J = 104
PL = 5 * J
EP = 2920
LAM = 0.4
LOOK = 4
CHUNKS = (0, 2, 4, 6, 8, 1, 3, 5, 7, 9)
WINDOWS = ((1, 2, 6, 7), (3, 4, 8, 9))
SLOT = (4, 0, 1, 2, 3)


def theta(n):
    return (4 * n) % 10


def seg_start(n):
    return (1024 * n - theta(n)) // 10


def seg_addr(n, c):
    t = theta(n)
    if c >= t:
        return J * ((c - t) // 2)
    return J * ((c - t + 10) // 2) - 1


def tile_kantlinear_kernel(tc, x, base_weight, cheby_weight, grad_out, out):
    nc = tc.nc
    with ExitStack() as ctx:
        const = ctx.enter_context(tc.tile_pool(name="const", bufs=1))
        rawp = ctx.enter_context(tc.tile_pool(name="rawp", bufs=3))
        grpp = ctx.enter_context(tc.tile_pool(name="grpp", bufs=3))
        keep = ctx.enter_context(tc.tile_pool(name="keep", bufs=1))
        wqp = ctx.enter_context(tc.tile_pool(name="wqp", bufs=2))
        upl = ctx.enter_context(tc.tile_pool(name="upl", bufs=4))
        hlp = ctx.enter_context(tc.tile_pool(name="hlp", bufs=2))
        otp = ctx.enter_context(tc.tile_pool(name="otp", bufs=2))
        tlp = ctx.enter_context(tc.tile_pool(name="tlp", bufs=1))
        pmx = ctx.enter_context(tc.psum_pool(name="pmx", bufs=5))
        pac = ctx.enter_context(tc.psum_pool(name="pac", bufs=1))
        ctx.enter_context(tc.manual_schedule())

        ident_f = const.tile([P, P], F32, name="ident_f")
        make_identity(nc, ident_f[:])
        ident_b = const.tile([P, P], BF16, name="ident_b")
        make_identity(nc, ident_b[:])

        w4 = cheby_weight.rearrange("o i k -> o (i k)").rearrange("(u q e) n -> q u e n", u=2, e=2)

        def load_w(it):
            raw = rawp.tile([P, 4, 1280], BF16, name="raw", tag="raw")
            for t in range(4):
                src = w4[:, t // 2, t % 2, :].rearrange("q (c f) -> q c f", c=10)
                dst = raw[:, t, :].rearrange("p (c f) -> p c f", c=10)
                for par in range(2):
                    nc.sync.dma_start(
                        out=dst[:, 5 * par : 5 * par + 5, :], in_=src[:, par:10:2, it * P : (it + 1) * P]
                    )
            return raw

        def regroup(dst, src, c0, c1, eng):
            d = dst[:, c0:c1, :].rearrange("p (c i) t -> p c t i", i=4)
            s = src[:, :, c0:c1].rearrange("p t (c i) -> p c t i", i=4)
            if eng == "v":
                nc.vector.tensor_copy(out=d, in_=s)
            else:
                nc.scalar.copy(out=d, in_=s)

        def quant(codes, scales, grp, c0, c1, fmt):
            nc.vector.quantize_mx(
                out=codes[:, c0:c1].bitcast(fmt),
                scales=scales[:, c0:c1],
                in_=grp[:, c0:c1, :].rearrange("p r t -> p (r t)"),
            )

        gs = rawp.tile([P, 8, 512], BF16, name="gs", tag="raw")
        for q in range(4):
            nc.sync.dma_start(
                out=gs[:, 2 * q : 2 * q + 2, :],
                in_=grad_out[256 * q : 256 * q + 256, :].rearrange("(t p) k -> p t k", p=P),
            )
        xs = rawp.tile([P, 10, 512], BF16, name="xs", tag="raw")
        nc.vector.memset(xs[96:128].bitcast(F32), 0.0)
        nc.sync.dma_start(out=xs[0:96], in_=x[0:960, :].rearrange("(j r) i -> j r i", r=10))
        nc.sync.dma_start(out=xs[96:102], in_=x[960:1020, :].rearrange("(j r) i -> j r i", r=10))
        nc.sync.dma_start(out=xs[102:103, 0:4, :], in_=x[1020:1024, :].rearrange("(o r) i -> o r i", o=1))
        raws = [load_w(0)]

        gn = grpp.tile([P, 1032, 4], BF16, name="gn", tag="grp", align_bytes=64)
        gn32 = gn[:].bitcast(F32)
        gs32 = gs[:].bitcast(F32)
        nc.vector.memset(gn32[:, 1024:1032, :], 0.0)
        for q in range(4):
            pt = pmx.tile([P, 2, 256], F32, name="ptg", tag="ps")
            for b in range(2):
                for u in range(2):
                    nc.tensor.transpose(
                        pt[:, u, b * P : (b + 1) * P], gs32[:, 2 * q + b, u * P : (u + 1) * P], ident_f[:]
                    )
            nc.scalar.copy(out=gn32[:, 256 * q : 256 * q + 256, :], in_=pt[:].rearrange("p u r -> p r u"))
        braw = rawp.tile([P, 4, 512], BF16, name="braw", tag="raw")
        nc.sync.dma_start(
            out=braw[:].rearrange("p (u e) n -> p u e n", u=2),
            in_=base_weight.rearrange("(u q e) n -> q u e n", u=2, e=2),
        )
        ge = grpp.tile([P, 1024, 4], BF16, name="ge", tag="grp", align_bytes=64)
        ge32 = ge[:].bitcast(F32)
        gw = grpp.tile([P, 1024, 4], BF16, name="gw", tag="grp", align_bytes=64)
        gw32 = gw[:].bitcast(F32)
        for wi, ns in enumerate(WINDOWS):
            for k, n in enumerate(ns):
                s = seg_start(n)
                nc.vector.tensor_copy(
                    out=gw32[:, 512 * wi + J * k : 512 * wi + J * k + J, :], in_=gn32[:, s : s + J, :]
                )
            nc.vector.tensor_copy(
                out=gw32[:, 512 * wi + 416 : 512 * wi + 468, :], in_=gn32[:, 512 + 52 * wi : 564 + 52 * wi, :]
            )
            nc.vector.memset(gw32[:, 512 * wi + 468 : 512 * wi + 512, :], 0.0)
        gcodes = keep.tile([P, 2048], U32, name="gcodes", align_bytes=64)
        gscales = keep.tile([P, 2048], U8, name="gscales", align_bytes=64)
        nc.vector.quantize_mx(
            out=gcodes[:, 1024:2048].bitcast(E5),
            scales=gscales[:, 1024:2048],
            in_=gw[:].rearrange("p r t -> p (r t)"),
        )
        for par in range(2):
            nc.vector.tensor_copy(out=ge32[:, 512 * par : 512 * par + 512, :], in_=gn32[:, par:1024:2, :])
        nc.vector.quantize_mx(
            out=gcodes[:, 0:1024].bitcast(E5),
            scales=gscales[:, 0:1024],
            in_=ge[:].rearrange("p r t -> p (r t)"),
        )

        xT = keep.tile([P, 40, J], BF16, name="xT")
        for grp in range(5):
            pt = pmx.tile([P, 8, P], BF16, name="ptx", tag="ps")
            for k in range(8):
                h, bp = divmod(8 * grp + k, 5)
                nc.tensor.transpose(
                    pt[:, k, :], xs[:, 2 * bp + h % 2, (h // 2) * P : (h // 2 + 1) * P], ident_b[:]
                )
            nc.scalar.copy(out=xT[:, 8 * grp : 8 * grp + 8, :], in_=pt[:, :, 0:J])
        raws.append(load_w(1))

        state = {}

        def pl(u, n):
            return u[:, n // 5, SLOT[n % 5] * PL : SLOT[n % 5] * PL + PL]

        def stage_sa(t):
            u = upl.tile([P, 2, EP], F32, name="u")
            xv = xT[:, 5 * t : 5 * t + 5, :].rearrange("p b j -> p (b j)")
            y2 = hlp.tile([P, PL], F32, name="y2")
            t2 = hlp.tile([P, PL], F32, name="t2")
            sg = hlp.tile([P, PL], F32, name="sg")
            sn = hlp.tile([P, PL], F32, name="sn")
            z3 = hlp.tile([P, PL], F32, name="z3")
            state[t] = {"u": u, "xv": xv, "y2": y2, "t2": t2, "sg": sg, "sn": sn, "z3": z3}
            nc.gpsimd.memset(u[:, :, 5 * PL : 5 * PL + 32], 0.0)
            nc.gpsimd.memset(pl(u, 0), 0.0)
            nc.scalar.activation(out=y2[:], in_=xv, func=ACT.Square, scale=math.sqrt(8.0))
            nc.scalar.activation(
                out=t2[:], in_=y2[:], func=ACT.Square, scale=math.sqrt(2.0) / 2.0, bias=-2.0 * math.sqrt(2.0)
            )
            nc.scalar.activation(out=sn[:], in_=xv, func=ACT.Sigmoid, scale=-1.0)
            nc.scalar.activation(out=pl(u, 2), in_=xv, func=ACT.Copy, scale=LAM)
            nc.scalar.activation(
                out=pl(u, 5), in_=y2[:], func=ACT.Square, scale=math.sqrt(0.5) / 2.0, bias=-1.5 * math.sqrt(0.5)
            )
            nc.scalar.activation(
                out=z3[:], in_=y2[:], func=ACT.Square, scale=math.sqrt(3.0) / 2.0, bias=-2.0 * math.sqrt(3.0)
            )
            nc.scalar.activation(out=sg[:], in_=xv, func=ACT.Sigmoid)
            nc.scalar.activation(out=pl(u, 1), in_=xv, func=ACT.Identity, scale=0.0, bias=0.1)

        def stage_ga(t):
            s = state[t]
            u = s["u"]
            vv = s["sn"]
            s["vv"] = vv
            nc.gpsimd.tensor_scalar(out=s["t2"][:], in0=s["t2"][:], scalar1=1.0, scalar2=-4.0, op0=ALU.mult, op1=ALU.add)
            nc.gpsimd.tensor_scalar(
                out=pl(u, 3), in0=s["y2"][:], scalar1=0.375 * LAM, scalar2=-0.75 * LAM, op0=ALU.mult, op1=ALU.add
            )
            nc.gpsimd.tensor_tensor(out=vv[:], in0=s["sn"][:], in1=s["xv"], op=ALU.mult)
            nc.gpsimd.tensor_tensor(out=pl(u, 7), in0=s["t2"][:], in1=pl(u, 3), op=ALU.mult)
            nc.gpsimd.tensor_scalar(
                out=pl(u, 7), in0=pl(u, 7), scalar1=7.0 / 6.0, scalar2=1.75 * LAM, op0=ALU.mult, op1=ALU.add
            )

        def stage_va(t, part):
            s = state[t]
            u = s["u"]
            if part == 0:
                nc.vector.scalar_tensor_tensor(
                    out=pl(u, 4), in0=s["y2"][:], scalar=4.0, in1=pl(u, 2), op0=ALU.subtract, op1=ALU.mult
                )
            elif part == 1:
                nc.vector.scalar_tensor_tensor(
                    out=pl(u, 9), in0=pl(u, 5), scalar=0.625, in1=s["t2"][:], op0=ALU.subtract, op1=ALU.mult
                )
            elif part == 2:
                nc.vector.scalar_tensor_tensor(
                    out=pl(u, 6), in0=s["z3"][:], scalar=3.0, in1=pl(u, 2), op0=ALU.subtract, op1=ALU.mult
                )
            else:
                sp = hlp.tile([P, PL], F32, name="sp")
                s["sp"] = sp
                nc.vector.scalar_tensor_tensor(
                    out=sp[:], in0=s["vv"][:], scalar=1.0, in1=s["sg"][:], op0=ALU.add, op1=ALU.mult
                )

        def stage_gb(t):
            s = state[t]
            u = s["u"]
            nc.gpsimd.tensor_tensor(out=pl(u, 8), in0=s["t2"][:], in1=pl(u, 4), op=ALU.mult)
            nc.gpsimd.tensor_scalar(
                out=pl(u, 9), in0=pl(u, 9), scalar1=2.25 * LAM, scalar2=-2.25 * LAM, op0=ALU.mult, op1=ALU.add
            )

        stage_sa(0)
        stage_ga(0)
        wcs = {}

        def new_w(it):
            grp = grpp.tile([P, 1280, 4], BF16, name="grp", tag="grp", align_bytes=64)
            wc = wqp.tile([P, 1280], U32, name="wc", align_bytes=64)
            ws = wqp.tile([P, 1280], U8, name="ws", align_bytes=64)
            wcs[it] = (wc, ws, grp)

        new_w(0)
        regroup(wcs[0][2], raws[0], 0, 512, "v")
        regroup(wcs[0][2], raws[0], 512, 1280, "s")
        quant(wcs[0][0], wcs[0][1], wcs[0][2], 0, 512, E4)
        for part in range(3):
            stage_va(0, part)
        stage_gb(0)
        quant(wcs[0][0], wcs[0][1], wcs[0][2], 512, 1024, E4)
        quant(wcs[0][0], wcs[0][1], wcs[0][2], 1024, 1280, E4)
        stage_va(0, 3)
        raws.append(load_w(2))
        stage_sa(1)
        stage_ga(1)
        bgrp = grpp.tile([P, 512, 4], BF16, name="bgrp", tag="grp", align_bytes=64)
        regroup(bgrp, braw, 0, 512, "s")
        bcodes = keep.tile([P, 512], U32, name="bcodes", align_bytes=64)
        bscales = keep.tile([P, 512], U8, name="bscales", align_bytes=64)
        raws.append(load_w(3))

        jobs = [(h, j) for h in range(8) for j in range(11)]
        banks = {}

        def emit_mx(h, j):
            ps = pmx.tile([P, 512], F32, name="ps", tag="ps")
            banks[(h, j)] = ps
            it, par = divmod(h, 2)
            if j == 10:
                codes, scales, col, g0 = bcodes, bscales, it * P, 512 * par
            else:
                codes, scales = wcs[it][0], wcs[it][1]
                col, g0 = (5 * par + j // 2) * P, 1024 + 512 * (j % 2)
            nc.tensor.matmul_mx(
                out=ps[:],
                lhsT=codes[:, col : col + P].bitcast(E4),
                lhsT_scale=scales[:, col : col + P],
                rhs=gcodes[:, g0 : g0 + 512].bitcast(E5),
                rhs_scale=gscales[:, g0 : g0 + 512],
                start=True,
                stop=True,
            )

        def consume(h, j):
            ps = banks[(h, j)]
            u = state[h]["u"]
            if j == 10:
                p0 = pl(u, 0).rearrange("p (b j) -> p b j", b=5)
                spv = state[h]["sp"][:].rearrange("p (b j) -> p b j", b=5)
                nc.vector.tensor_tensor(
                    out=p0[:, :, 0:102],
                    in0=spv[:, :, 0:102],
                    in1=ps[:, 0:510].rearrange("p (j b) -> p b j", b=5),
                    op=ALU.mult,
                )
                nc.vector.tensor_tensor(
                    out=p0[:, 0:2, 102:103],
                    in0=spv[:, 0:2, 102:103],
                    in1=ps[:, 510:512].rearrange("p (j b) -> p b j", b=2),
                    op=ALU.mult,
                )
                return
            c = 2 * (j // 2) + h % 2
            wi = j % 2
            na, nb = WINDOWS[wi][0], WINDOWS[wi][1]
            aa = SLOT[na] * PL + seg_addr(na, c)
            step = SLOT[nb] * PL + seg_addr(nb, c) - aa
            dst = u[:, :, aa : aa + 2 * step].rearrange("p e (a d) -> p e a d", a=2)[:, :, :, 0:J]
            src = ps[:, 0 : 4 * J].rearrange("p (e a j) -> p e a j", e=2, a=2)
            nc.vector.tensor_tensor(out=dst, in0=dst, in1=src, op=ALU.mult)
            a = SLOT[0] * PL + seg_addr(5, c) + 52 * wi
            d5 = u[:, 1, a : a + 52]
            nc.vector.scalar_tensor_tensor(
                out=d5, in0=d5, scalar=0.625, in1=ps[:, 416:468], op0=ALU.subtract, op1=ALU.mult
            )

        acc = {}
        order = [(n, b) for n in range(10) for b in (0, 1, 2)] + [(n, b) for n in range(10) for b in (3, 4)]
        cuts = (0, 15, 30, 40, 50)

        def bunch(h, i, todo=None, summed=None):
            u = state[h]["u"]
            if i == 0:
                acc[h] = [pac.tile([P, 2, P], F32, name="pa%d" % b) for b in range(3)]
                state[h]["ot"] = otp.tile([P, 5, P], F32, name="ot")
            pas = acc[h]
            for n, bp in order[cuts[i] : cuts[i + 1]] if todo is None else todo:
                a = (n % 5) * PL + J * bp
                nc.tensor.matmul(
                    out=pas[bp % 3][:, bp // 3, :],
                    lhsT=u[:, n // 5, a : a + P] if summed is None else summed[:, 0, J * (bp - 2) : J * (bp - 2) + P],
                    rhs=ident_f[:],
                    is_transpose=True,
                    start=(n == 0),
                    stop=(n == 9 or summed is not None),
                )
            ot = state[h]["ot"]
            if i == 1:
                nc.scalar.copy(out=ot[:, 2:3, :], in_=pas[2][:, 0:1, :])
            if i == 3:
                nc.scalar.copy(out=ot[:, 0:4:3, :], in_=pas[0][:])
                nc.scalar.copy(out=ot[:, 1:5:3, :], in_=pas[1][:])
                it, par = divmod(h, 2)
                cols = slice(it * P, (it + 1) * P)
                nc.sync.dma_start(
                    out=out[0:960, cols].rearrange("(j r) i -> j r i", r=10)[:, par:10:2, :], in_=ot[0:96]
                )
                nc.sync.dma_start(
                    out=out[960:1020, cols].rearrange("(j r) i -> j r i", r=10)[:, par:10:2, :], in_=ot[96:102]
                )
                nc.sync.dma_start(
                    out=out[1020:1024, cols].rearrange("(o r) i -> o r i", o=1)[:, par:4:2, :],
                    in_=ot[102:103, 0:2, :],
                )

        for q in range(-LOOK, len(jobs)):
            if q == -LOOK:
                quant(bcodes, bscales, bgrp, 0, 512, E4)
            if q + LOOK < len(jobs):
                emit_mx(*jobs[q + LOOK])
            if q < 0:
                continue
            h, j = jobs[q]
            consume(h, j)
            it, par = divmod(h, 2)
            if j == 0 and h + 2 < 8:
                stage_sa(h + 2)
            if h + 1 < 8:
                if j in (1, 3, 5, 7):
                    stage_va(h + 1, (j - 1) // 2)
                if j == 4:
                    stage_gb(h + 1)
            if j == 6 and h + 2 < 8:
                stage_ga(h + 2)
            if it < 3:
                if par == 0 and j == 2:
                    new_w(it + 1)
                    regroup(wcs[it + 1][2], raws[it + 1], 0, 640, "s")
                if par == 0 and j == 7:
                    regroup(wcs[it + 1][2], raws[it + 1], 640, 1280, "s")
                if par == 1 and j in (0, 2, 4):
                    c0, c1 = ((0, 512), (512, 1024), (1024, 1280))[j // 2]
                    quant(wcs[it + 1][0], wcs[it + 1][1], wcs[it + 1][2], c0, c1, E4)
            if h > 0 and j in (1, 3, 5, 7):
                bunch(h - 1, (j - 1) // 2)
        ul = state[7]["u"][:, :, 0 : 5 * PL].rearrange("p e (v r) -> p e v r", v=5)
        lo = 2 * J
        wd = PL - lo
        sc = tlp.tile([P, 5, wd + 32], F32, name="sc")
        nc.vector.memset(sc[:, 0, wd : wd + 32], 0.0)
        nc.vector.tensor_tensor(out=sc[:, :, 0:wd], in0=ul[:, 0, :, lo:PL], in1=ul[:, 1, :, lo:PL], op=ALU.add)
        nc.vector.tensor_tensor(out=sc[:, 0:4:2, 0:wd], in0=sc[:, 0:4:2, 0:wd], in1=sc[:, 1:4:2, 0:wd], op=ALU.add)
        nc.vector.tensor_tensor(out=sc[:, 0, 0:wd], in0=sc[:, 0, 0:wd], in1=sc[:, 2, 0:wd], op=ALU.add)
        nc.vector.tensor_tensor(out=sc[:, 0, 0:wd], in0=sc[:, 0, 0:wd], in1=sc[:, 4, 0:wd], op=ALU.add)
        bunch(7, 0, [(n, b) for n in range(10) for b in (0, 1)])
        bunch(7, 1, [(0, 2)], sc)
        bunch(7, 3, [(0, 3), (0, 4)], sc)
